import numpy as np
import ml_dtypes


def mxq(x, axis, fmt="e4m3"):
    dtype, down = {"e4m3": (ml_dtypes.float8_e4m3fn, 7), "e5m2": (ml_dtypes.float8_e5m2, 14)}[fmt]
    v = np.moveaxis(np.asarray(x, np.float32).astype(ml_dtypes.bfloat16).astype(np.float64), axis, -1)
    blocks = v.reshape(v.shape[:-1] + (-1, 32))
    amax = np.abs(blocks).max(-1, keepdims=True)
    byte = np.maximum(np.where(amax > 0, np.frexp(amax)[1] - 1 + 127, 0) - down, 1)
    scale = np.exp2(byte - 127.0)
    codes = (blocks / scale).astype(np.float32).astype(dtype).astype(np.float64)
    return np.moveaxis((codes * scale).reshape(v.shape), -1, axis)


WIDE = False


def mx_kscale(k):
    if not WIDE:
        return np.ones(k)
    levels = np.array([10, -10, 5, -5, 0])
    a = np.random.permutation(np.resize(levels, k // 512 * 4)).reshape(k // 512, 4)
    idx = np.arange(k)
    return np.exp2(a[idx // 512, idx % 128 // 32])


BF16 = ml_dtypes.bfloat16


def bf(x):
    return np.asarray(x, np.float32).astype(BF16)


def f64(x):
    return np.asarray(x).astype(np.float64)


B, C, HH, WW, D, MH, MW, F, G = 8, 1024, 32, 32, 128, 32, 16, 512, 64
N = B * HH * WW
EPS = 1e-12
VT = 0.5
PA = 3.0


def l2norm(v):
    return v / np.maximum(np.sqrt(np.sum(v * v, axis=-1, keepdims=True)), EPS)


def setup_inputs():
    t = mx_kscale(F)
    gp = PA / (PA + np.arange(D))
    return {"z": bf(np.random.standard_normal((B, C, HH, WW)) * (0.5 + np.random.random((B, 1, HH, WW)))),
            "Wq1": bf(np.random.standard_normal((C, F)) * t),
            "bq1": bf(np.random.standard_normal(F) * 0.1 * t),
            "Wq2": bf(np.random.standard_normal((F, D)) * gp * np.sqrt(VT * D / (0.5 * F * np.sum(gp * gp))) / t[:, None]),
            "bq2": bf(np.random.standard_normal(D) * 0.1)}


def reference(z, Wq1, bq1, Wq2, bq2):
    x = f64(z).transpose(0, 2, 3, 1).reshape(N, C)
    xn = l2norm(x)
    h = np.maximum((mxq(xn, 1, "e4m3") @ mxq(f64(Wq1), 0, "e4m3")) + f64(bq1), 0.0)
    Zq = (mxq(h, 1, "e4m3") @ mxq(f64(Wq2), 0, "e4m3")) + f64(bq2)
    mu_z = Zq.mean(axis=1, keepdims=True)
    var_z = Zq.var(axis=1, ddof=1, keepdims=True)
    Zc = l2norm(Zq - mu_z)
    return Zc, var_z

@@ -1,0 +1,276 @@
+from contextlib import ExitStack
+
+import concourse.mybir as mybir
+from concourse.masks import make_identity
+
+BF16 = mybir.dt.bfloat16
+F32 = mybir.dt.float32
+U32 = mybir.dt.uint32
+U8 = mybir.dt.uint8
+FP8X4 = mybir.dt.float8_e4m3fn_x4
+ACT = mybir.ActivationFunctionType
+ALU = mybir.AluOpType
+
+P = 128
+PACK = 4
+BATCH, CHANNELS, PIXELS = 8, 1024, 1024
+HIDDEN, FEATURES = 512, 128
+PASSES = CHANNELS // (P * PACK)
+F_TILES = HIDDEN // P
+GROUP = 512
+TILES = GROUP // P
+GROUPS = BATCH * PIXELS // GROUP
+EPS_SQUARED = 1e-24
+
+FLOPS = 2 * BATCH * PIXELS * (CHANNELS * HIDDEN + HIDDEN * FEATURES)
+
+
+def tile_spatialmemorymodule_pb_kernel(tc, z, Wq1, bq1, Wq2, bq2, out_0, out_1):
+    nc = tc.nc
+    with ExitStack() as ctx:
+        const = ctx.enter_context(tc.tile_pool(name="const", bufs=1))
+        xpool = ctx.enter_context(tc.tile_pool(name="xpool", bufs=BATCH))
+        work = ctx.enter_context(tc.tile_pool(name="work", bufs=2))
+        codes = ctx.enter_context(tc.tile_pool(name="codes", bufs=3))
+        small = ctx.enter_context(tc.tile_pool(name="small", bufs=4))
+        ps_t = ctx.enter_context(tc.psum_pool(name="ps_t", bufs=2))
+        ps_r = ctx.enter_context(tc.psum_pool(name="ps_r", bufs=2))
+        ps_h = ctx.enter_context(tc.psum_pool(name="ps_h", bufs=3))
+        ps_z = ctx.enter_context(tc.psum_pool(name="ps_z", bufs=1))
+
+        x_all = []
+
+        def load_batch(b):
+            x_sb = xpool.tile([P, PASSES, PACK, PIXELS], BF16, name="x_sb")
+            src = z[b].rearrange("(g p j) h w -> p g (j h w)", g=PASSES, j=PACK)
+            for g in range(PASSES):
+                nc.sync.dma_start(
+                    out=x_sb[:, g].rearrange("p j n -> p (j n)"), in_=src[:, g, :]
+                )
+            x_all.append(x_sb)
+
+        load_batch(0)
+        w1_raw = work.tile([P, PASSES, PACK, HIDDEN], BF16, tag="grouped_x", align_bytes=64)
+        nc.sync.dma_start(
+            out=w1_raw[:].rearrange("p g j f -> p g (j f)"),
+            in_=Wq1.rearrange("(g p j) f -> p g (j f)", g=PASSES, j=PACK),
+        )
+        w2_raw = const.tile([P, PACK, FEATURES], BF16)
+        nc.sync.dma_start(out=w2_raw[:], in_=Wq2.rearrange("(t p) d -> p t d", p=P))
+        b1_rows = const.tile([P, P], BF16)
+        nc.vector.memset(b1_rows[:], 0.0)
+        nc.sync.dma_start(out=b1_rows[0:F_TILES, :], in_=bq1.rearrange("(t p) -> t p", p=P))
+        b2_bf = const.tile([P, FEATURES], BF16)
+        nc.sync.dma_start(out=b2_bf[:], in_=bq2.partition_broadcast(P))
+        for b in range(1, BATCH):
+            load_batch(b)
+
+        ident_bf = const.tile([P, P], BF16)
+        make_identity(nc, ident_bf[:])
+        ident_f = const.tile([P, P], F32)
+        make_identity(nc, ident_f[:])
+        var_all = const.tile([P, P], F32)
+        nc.vector.memset(var_all[:], 0.0)
+
+        w1_grouped = work.tile([P, PASSES, HIDDEN, PACK], BF16, tag="grouped_x", align_bytes=64)
+        w1_codes = const.tile([P, PASSES, HIDDEN], U32, align_bytes=64)
+        w1_scales = const.tile([P, PASSES, HIDDEN], U8, align_bytes=64)
+        for g in range(PASSES):
+            nc.vector.tensor_copy(
+                out=w1_grouped[:, g], in_=w1_raw[:, g].rearrange("p j f -> p f j")
+            )
+        w2_grouped = const.tile([P, FEATURES, PACK], BF16, align_bytes=64)
+        nc.vector.tensor_copy(out=w2_grouped[:], in_=w2_raw[:].rearrange("p t d -> p d t"))
+        for g in range(PASSES):
+            nc.vector.quantize_mx(
+                out=w1_codes[:, g, :].bitcast(FP8X4),
+                scales=w1_scales[:, g, :],
+                in_=w1_grouped[:, g].rearrange("p f j -> p (f j)"),
+            )
+        w2_codes = const.tile([P, FEATURES], U32, align_bytes=64)
+        w2_scales = const.tile([P, FEATURES], U8, align_bytes=64)
+        nc.vector.quantize_mx(
+            out=w2_codes[:].bitcast(FP8X4),
+            scales=w2_scales[:],
+            in_=w2_grouped[:].rearrange("p d t -> p (d t)"),
+        )
+
+        b1_t = ps_z.tile([P, P], BF16, tag="z_acc")
+        nc.tensor.transpose(b1_t[:], b1_rows[:], ident_bf[:])
+        b1_cols = const.tile([P, F_TILES], F32)
+        nc.vector.tensor_copy(out=b1_cols[:], in_=b1_t[:, 0:F_TILES])
+        b2_f = const.tile([P, FEATURES], F32)
+        nc.vector.tensor_copy(out=b2_f[:], in_=b2_bf[:])
+
+        live = {}
+
+        def token_norms(s):
+            x_sb = x_all[s // 2]
+            first = (s % 2) * GROUP
+            norm_sq = small.tile([P, TILES], F32, name="norm_sq")
+            for i in range(TILES):
+                cols = slice(first + i * P, first + (i + 1) * P)
+                x_t = ps_t.tile([P, PASSES * PACK, P], BF16, name="x_t")
+                for g in range(PASSES):
+                    for j in range(PACK):
+                        nc.tensor.transpose(x_t[:, g * PACK + j, :], x_sb[:, g, j, cols], ident_bf[:])
+                squares = work.tile([P, CHANNELS], BF16, name="squares")
+                nc.scalar.activation(
+                    out=squares[:],
+                    in_=x_t[:].rearrange("p a k -> p (a k)"),
+                    func=ACT.Square,
+                    accum_out=norm_sq[:, i : i + 1],
+                )
+            live["norm_sq", s] = norm_sq
+
+        def spread_inverse_norms(s):
+            norm_sq = live.pop(("norm_sq", s))
+            clamped = small.tile([P, TILES], F32, name="clamped")
+            nc.vector.tensor_scalar_max(out=clamped[:], in0=norm_sq[:], scalar1=EPS_SQUARED)
+            norm = small.tile([P, TILES], F32, name="norm")
+            nc.scalar.activation(out=norm[:], in_=clamped[:], func=ACT.Sqrt)
+            inv_norm = small.tile([P, TILES], F32, name="inv_norm")
+            nc.vector.reciprocal(out=inv_norm[:], in_=norm[:])
+            inv_row = ps_r.tile([P, GROUP], F32, name="inv_row")
+            for i in range(TILES):
+                nc.tensor.matmul(
+                    inv_row[:, i * P : (i + 1) * P],
+                    lhsT=inv_norm[:, i : i + 1].to_broadcast([P, P]),
+                    rhs=ident_f[:],
+                    start=True,
+                    stop=True,
+                )
+            live["inv_row", s] = inv_row
+
+        def normalise_and_quantise(s):
+            x_sb = x_all[s // 2]
+            cols = slice((s % 2) * GROUP, (s % 2 + 1) * GROUP)
+            inv_row = live.pop(("inv_row", s))
+            grouped_x = work.tile([P, PASSES, GROUP, PACK], BF16, name="grouped_x", align_bytes=64)
+            x_codes = codes.tile([P, PASSES, GROUP], U32, name="x_codes", align_bytes=64)
+            x_scales = codes.tile([P, PASSES, GROUP], U8, name="x_scales", align_bytes=64)
+            for g in range(PASSES):
+                nc.vector.tensor_tensor(
+                    out=grouped_x[:, g],
+                    in0=x_sb[:, g, :, cols].rearrange("p j n -> p n j"),
+                    in1=inv_row[:].unsqueeze(2).to_broadcast([P, GROUP, PACK]),
+                    op=ALU.mult,
+                )
+            for g in range(PASSES):
+                nc.vector.quantize_mx(
+                    out=x_codes[:, g, :].bitcast(FP8X4),
+                    scales=x_scales[:, g, :],
+                    in_=grouped_x[:, g].rearrange("p n j -> p (n j)"),
+                )
+            live["x", s] = (x_codes, x_scales)
+
+        def hidden_layer(s):
+            x_codes, x_scales = live.pop(("x", s))
+            h_planes = work.tile([P, F_TILES, GROUP], BF16, name="h_planes")
+            for t in range(F_TILES):
+                f_cols = slice(t * P, (t + 1) * P)
+                h_acc = ps_h.tile([P, GROUP], F32, name="h_acc")
+                for g in range(PASSES):
+                    nc.tensor.matmul_mx(
+                        out=h_acc[:],
+                        lhsT=w1_codes[:, g, f_cols].bitcast(FP8X4),
+                        lhsT_scale=w1_scales[:, g, f_cols],
+                        rhs=x_codes[:, g, :].bitcast(FP8X4),
+                        rhs_scale=x_scales[:, g, :],
+                        start=(g == 0),
+                        stop=(g == PASSES - 1),
+                    )
+                nc.scalar.activation(
+                    out=h_planes[:, t, :], in_=h_acc[:], func=ACT.Relu, bias=b1_cols[:, t : t + 1]
+                )
+            grouped_h = work.tile([P, GROUP, PACK], BF16, name="grouped_h", align_bytes=64)
+            nc.vector.tensor_copy(out=grouped_h[:], in_=h_planes[:].rearrange("p t n -> p n t"))
+            h_codes = codes.tile([P, GROUP], U32, name="h_codes", align_bytes=64)
+            h_scales = codes.tile([P, GROUP], U8, name="h_scales", align_bytes=64)
+            nc.vector.quantize_mx(
+                out=h_codes[:].bitcast(FP8X4),
+                scales=h_scales[:],
+                in_=grouped_h[:].rearrange("p n t -> p (n t)"),
+            )
+            live["h", s] = (h_codes, h_scales)
+
+        def codes_and_statistics(s):
+            h_codes, h_scales = live.pop(("h", s))
+            z_acc = ps_z.tile([P, TILES, FEATURES], F32, name="z_acc")
+            for i in range(TILES):
+                rows = slice(i * P, (i + 1) * P)
+                nc.tensor.matmul_mx(
+                    out=z_acc[:, i, :],
+                    lhsT=h_codes[:, rows].bitcast(FP8X4),
+                    lhsT_scale=h_scales[:, rows],
+                    rhs=w2_codes[:].bitcast(FP8X4),
+                    rhs_scale=w2_scales[:],
+                    start=True,
+                    stop=True,
+                )
+            zq = work.tile([P, TILES, FEATURES], F32, name="zq")
+            nc.vector.tensor_tensor(
+                out=zq[:],
+                in0=z_acc[:],
+                in1=b2_f[:].unsqueeze(1).to_broadcast([P, TILES, FEATURES]),
+                op=ALU.add,
+            )
+            stats = small.tile([P, TILES, 6], F32, name="stats")
+            mean_var = small.tile([P, TILES, 2], F32, name="mean_var")
+            for i in range(TILES):
+                nc.vector.bn_stats(out=stats[:, i, :], in_=zq[:, i, :])
+            for i in range(TILES):
+                nc.vector.bn_aggr(out=mean_var[:, i, :], in_=stats[:, i, :])
+            sum_sq = small.tile([P, TILES], F32, name="sum_sq")
+            nc.vector.tensor_scalar(
+                out=sum_sq[:],
+                in0=mean_var[:, :, 1],
+                scalar1=float(FEATURES),
+                scalar2=EPS_SQUARED,
+                op0=ALU.mult,
+                op1=ALU.max,
+            )
+            nc.vector.tensor_scalar_mul(
+                out=var_all[:, s * TILES : (s + 1) * TILES],
+                in0=mean_var[:, :, 1],
+                scalar1=FEATURES / (FEATURES - 1.0),
+            )
+            length = small.tile([P, TILES], F32, name="length")
+            nc.scalar.activation(out=length[:], in_=sum_sq[:], func=ACT.Sqrt)
+            inv_length = small.tile([P, TILES], F32, name="inv_length")
+            nc.vector.reciprocal(out=inv_length[:], in_=length[:])
+            zc = work.tile([P, TILES, FEATURES], F32, name="zc")
+            for i in range(TILES):
+                nc.vector.tensor_scalar(
+                    out=zc[:, i, :],
+                    in0=zq[:, i, :],
+                    scalar1=mean_var[:, i, 0:1],
+                    scalar2=inv_length[:, i : i + 1],
+                    op0=ALU.subtract,
+                    op1=ALU.mult,
+                )
+            nc.sync.dma_start(
+                out=out_0[s * GROUP : (s + 1) * GROUP, :].rearrange("(i p) d -> p i d", p=P),
+                in_=zc[:],
+            )
+
+        stages = [
+            token_norms,
+            spread_inverse_norms,
+            normalise_and_quantise,
+            hidden_layer,
+            codes_and_statistics,
+        ]
+        for step in range(GROUPS + len(stages) - 1):
+            for lag, stage in enumerate(stages):
+                if 0 <= step - lag < GROUPS:
+                    stage(step - lag)
+
+        var_t = ps_z.tile([P, P], F32, tag="z_acc")
+        nc.tensor.transpose(var_t[:], var_all[:], ident_f[:])
+        var_rows = const.tile([P, P], F32)
+        nc.vector.tensor_copy(out=var_rows[:], in_=var_t[:])
+        token_tiles = GROUPS * TILES
+        nc.sync.dma_start(
+            out=out_1.rearrange("(c p) o -> c (p o)", p=P), in_=var_rows[0:token_tiles, :]
+        )

@@ -20,7 +20,13 @@ F_TILES = HIDDEN // P
 GROUP = 512
 TILES = GROUP // P
 GROUPS = BATCH * PIXELS // GROUP
+GROUPS_PER_IMAGE = PIXELS // GROUP
 EPS_SQUARED = 1e-24
+RUN = 4
+PAIR = 2
+BLOCKS = GROUP // (PAIR * P)
+AHEAD = 2
+DEEPEST_LAG = 5
 
 FLOPS = 2 * BATCH * PIXELS * (CHANNELS * HIDDEN + HIDDEN * FEATURES)
 
@@ -29,189 +35,202 @@ def tile_spatialmemorymodule_pb_kernel(tc, z, Wq1, bq1, Wq2, bq2, out_0, out_1):
     nc = tc.nc
     with ExitStack() as ctx:
         const = ctx.enter_context(tc.tile_pool(name="const", bufs=1))
-        xpool = ctx.enter_context(tc.tile_pool(name="xpool", bufs=BATCH))
+        xpool = ctx.enter_context(tc.tile_pool(name="xpool", bufs=GROUPS))
         work = ctx.enter_context(tc.tile_pool(name="work", bufs=2))
-        codes = ctx.enter_context(tc.tile_pool(name="codes", bufs=3))
+        late = ctx.enter_context(tc.tile_pool(name="late", bufs=3))
         small = ctx.enter_context(tc.tile_pool(name="small", bufs=4))
-        ps_t = ctx.enter_context(tc.psum_pool(name="ps_t", bufs=2))
-        ps_r = ctx.enter_context(tc.psum_pool(name="ps_r", bufs=2))
+        ps_t = ctx.enter_context(tc.psum_pool(name="ps_t", bufs=3))
+        ps_r = ctx.enter_context(tc.psum_pool(name="ps_r", bufs=1))
         ps_h = ctx.enter_context(tc.psum_pool(name="ps_h", bufs=3))
         ps_z = ctx.enter_context(tc.psum_pool(name="ps_z", bufs=1))
 
+        def regroup(engine_copy, dst, src):
+            engine_copy(
+                out=dst.rearrange("p (c i) t -> p c t i", i=RUN),
+                in_=src.rearrange("p t (c i) -> p c t i", i=RUN),
+            )
+
+        def quantise(words, scales, grouped):
+            nc.vector.quantize_mx(
+                out=words.bitcast(FP8X4), scales=scales, in_=grouped.rearrange("p c t -> p (c t)")
+            )
+
         x_all = []
 
-        def load_batch(b):
-            x_sb = xpool.tile([P, PASSES, PACK, PIXELS], BF16, name="x_sb")
-            src = z[b].rearrange("(g p j) h w -> p g (j h w)", g=PASSES, j=PACK)
+        def load_group(s):
+            x_sb = xpool.tile([P, PASSES, PACK, GROUP], BF16, name="x_sb")
+            image = z[s // GROUPS_PER_IMAGE].rearrange(
+                "(g p j) h w -> p g j (h w)", g=PASSES, j=PACK
+            )
+            first = (s % GROUPS_PER_IMAGE) * GROUP
             for g in range(PASSES):
-                nc.sync.dma_start(
-                    out=x_sb[:, g].rearrange("p j n -> p (j n)"), in_=src[:, g, :]
-                )
+                nc.sync.dma_start(out=x_sb[:, g], in_=image[:, g, :, first : first + GROUP])
             x_all.append(x_sb)
 
-        load_batch(0)
+        b1_rows = const.tile([P, P], BF16)
+        nc.vector.memset(b1_rows[:], 0.0)
+        load_group(0)
+        nc.sync.dma_start(out=b1_rows[0:F_TILES, :], in_=bq1.rearrange("(t p) -> t p", p=P))
+        b2_bf = const.tile([P, FEATURES], BF16)
+        nc.sync.dma_start(out=b2_bf[:], in_=bq2.partition_broadcast(P))
+        w2_raw = const.tile([P, PACK, FEATURES], BF16)
+        nc.sync.dma_start(out=w2_raw[:], in_=Wq2.rearrange("(t p) d -> p t d", p=P))
         w1_raw = work.tile([P, PASSES, PACK, HIDDEN], BF16, tag="grouped_x", align_bytes=64)
         nc.sync.dma_start(
             out=w1_raw[:].rearrange("p g j f -> p g (j f)"),
             in_=Wq1.rearrange("(g p j) f -> p g (j f)", g=PASSES, j=PACK),
         )
-        w2_raw = const.tile([P, PACK, FEATURES], BF16)
-        nc.sync.dma_start(out=w2_raw[:], in_=Wq2.rearrange("(t p) d -> p t d", p=P))
-        b1_rows = const.tile([P, P], BF16)
-        nc.vector.memset(b1_rows[:], 0.0)
-        nc.sync.dma_start(out=b1_rows[0:F_TILES, :], in_=bq1.rearrange("(t p) -> t p", p=P))
-        b2_bf = const.tile([P, FEATURES], BF16)
-        nc.sync.dma_start(out=b2_bf[:], in_=bq2.partition_broadcast(P))
-        for b in range(1, BATCH):
-            load_batch(b)
+        for s in range(1, GROUPS):
+            load_group(s)
 
         ident_bf = const.tile([P, P], BF16)
         make_identity(nc, ident_bf[:])
         ident_f = const.tile([P, P], F32)
         make_identity(nc, ident_f[:])
-        var_all = const.tile([P, P], F32)
+        var_all = const.tile([P, PAIR, P], F32)
         nc.vector.memset(var_all[:], 0.0)
-
-        w1_grouped = work.tile([P, PASSES, HIDDEN, PACK], BF16, tag="grouped_x", align_bytes=64)
-        w1_codes = const.tile([P, PASSES, HIDDEN], U32, align_bytes=64)
-        w1_scales = const.tile([P, PASSES, HIDDEN], U8, align_bytes=64)
-        for g in range(PASSES):
-            nc.vector.tensor_copy(
-                out=w1_grouped[:, g], in_=w1_raw[:, g].rearrange("p j f -> p f j")
-            )
-        w2_grouped = const.tile([P, FEATURES, PACK], BF16, align_bytes=64)
-        nc.vector.tensor_copy(out=w2_grouped[:], in_=w2_raw[:].rearrange("p t d -> p d t"))
-        for g in range(PASSES):
-            nc.vector.quantize_mx(
-                out=w1_codes[:, g, :].bitcast(FP8X4),
-                scales=w1_scales[:, g, :],
-                in_=w1_grouped[:, g].rearrange("p f j -> p (f j)"),
-            )
-        w2_codes = const.tile([P, FEATURES], U32, align_bytes=64)
-        w2_scales = const.tile([P, FEATURES], U8, align_bytes=64)
-        nc.vector.quantize_mx(
-            out=w2_codes[:].bitcast(FP8X4),
-            scales=w2_scales[:],
-            in_=w2_grouped[:].rearrange("p d t -> p (d t)"),
-        )
-
-        b1_t = ps_z.tile([P, P], BF16, tag="z_acc")
-        nc.tensor.transpose(b1_t[:], b1_rows[:], ident_bf[:])
-        b1_cols = const.tile([P, F_TILES], F32)
-        nc.vector.tensor_copy(out=b1_cols[:], in_=b1_t[:, 0:F_TILES])
-        b2_f = const.tile([P, FEATURES], F32)
-        nc.vector.tensor_copy(out=b2_f[:], in_=b2_bf[:])
+        one = const.tile([P, 1], F32)
+        nc.vector.memset(one[:], 1.0)
+        nc.scalar.activation(out=one[:], in_=one[:], func=ACT.Sqrt)
 
         live = {}
 
-        def token_norms(s):
-            x_sb = x_all[s // 2]
-            first = (s % 2) * GROUP
-            norm_sq = small.tile([P, TILES], F32, name="norm_sq")
-            for i in range(TILES):
-                cols = slice(first + i * P, first + (i + 1) * P)
-                x_t = ps_t.tile([P, PASSES * PACK, P], BF16, name="x_t")
-                for g in range(PASSES):
-                    for j in range(PACK):
-                        nc.tensor.transpose(x_t[:, g * PACK + j, :], x_sb[:, g, j, cols], ident_bf[:])
-                squares = work.tile([P, CHANNELS], BF16, name="squares")
+        def transposes(u):
+            s, b, g = u // TILES, u % TILES // PASSES, u % PASSES
+            words = x_all[s][:].bitcast(F32)
+            x_t = ps_t.tile([P, PACK, P], F32, name="x_t")
+            for j in range(PACK):
+                nc.tensor.transpose(x_t[:, j, :], words[:, g, j, b * P : (b + 1) * P], ident_f[:])
+            live["x_t", u] = x_t
+
+        def squares(u):
+            s, b, g = u // TILES, u % TILES // PASSES, u % PASSES
+            if u % TILES == 0:
+                live["norm_parts", s] = small.tile([P, PAIR, BLOCKS, PASSES], F32, name="norm_parts")
+            halves = live.pop(("x_t", u))[:].bitcast(BF16).rearrange("p j (k e) -> p e j k", e=PAIR)
+            for e in range(PAIR):
+                unused = work.tile([P, PACK, P], BF16, name="unused")
                 nc.scalar.activation(
-                    out=squares[:],
-                    in_=x_t[:].rearrange("p a k -> p (a k)"),
+                    out=unused[:],
+                    in_=halves[:, e],
                     func=ACT.Square,
-                    accum_out=norm_sq[:, i : i + 1],
+                    accum_out=live["norm_parts", s][:, e, b, g : g + 1],
                 )
+
+        def add_passes(s):
+            norm_sq = small.tile([P, TILES], F32, name="norm_sq")
+            nc.vector.tensor_reduce(
+                out=norm_sq[:],
+                in_=live.pop(("norm_parts", s))[:].rearrange("p e b g -> p (e b) g"),
+                axis=mybir.AxisListType.X,
+                op=ALU.add,
+            )
             live["norm_sq", s] = norm_sq
 
-        def spread_inverse_norms(s):
-            norm_sq = live.pop(("norm_sq", s))
-            clamped = small.tile([P, TILES], F32, name="clamped")
-            nc.vector.tensor_scalar_max(out=clamped[:], in0=norm_sq[:], scalar1=EPS_SQUARED)
+        def clamped_root(out, in_, scale):
+            above = small.tile([P, TILES], F32, name="above")
+            nc.scalar.activation(out=above[:], in_=in_, func=ACT.Relu, scale=scale, bias=-EPS_SQUARED)
+            nc.scalar.activation(out=out, in_=above[:], func=ACT.Sqrt, bias=EPS_SQUARED)
+
+        def norms(s):
             norm = small.tile([P, TILES], F32, name="norm")
-            nc.scalar.activation(out=norm[:], in_=clamped[:], func=ACT.Sqrt)
+            clamped_root(norm[:], live.pop(("norm_sq", s))[:], 1.0)
+            live["norm", s] = norm
+
+        def invert_norms(s):
             inv_norm = small.tile([P, TILES], F32, name="inv_norm")
-            nc.vector.reciprocal(out=inv_norm[:], in_=norm[:])
+            nc.vector.reciprocal(out=inv_norm[:], in_=live.pop(("norm", s))[:])
+            live["inv_norm", s] = inv_norm
+
+        def spread_inverse_norms(s):
+            inv_norm = live.pop(("inv_norm", s))
             inv_row = ps_r.tile([P, GROUP], F32, name="inv_row")
             for i in range(TILES):
-                nc.tensor.matmul(
+                nc.tensor.transpose(
                     inv_row[:, i * P : (i + 1) * P],
-                    lhsT=inv_norm[:, i : i + 1].to_broadcast([P, P]),
-                    rhs=ident_f[:],
-                    start=True,
-                    stop=True,
+                    inv_norm[:, i : i + 1].to_broadcast([P, P]),
+                    ident_f[:],
                 )
             live["inv_row", s] = inv_row
 
-        def normalise_and_quantise(s):
-            x_sb = x_all[s // 2]
-            cols = slice((s % 2) * GROUP, (s % 2 + 1) * GROUP)
+        def normalise(s):
             inv_row = live.pop(("inv_row", s))
             grouped_x = work.tile([P, PASSES, GROUP, PACK], BF16, name="grouped_x", align_bytes=64)
-            x_codes = codes.tile([P, PASSES, GROUP], U32, name="x_codes", align_bytes=64)
-            x_scales = codes.tile([P, PASSES, GROUP], U8, name="x_scales", align_bytes=64)
             for g in range(PASSES):
                 nc.vector.tensor_tensor(
-                    out=grouped_x[:, g],
-                    in0=x_sb[:, g, :, cols].rearrange("p j n -> p n j"),
-                    in1=inv_row[:].unsqueeze(2).to_broadcast([P, GROUP, PACK]),
+                    out=grouped_x[:, g].rearrange("p (e n) j -> p e n j", e=PAIR),
+                    in0=x_all[s][:, g].rearrange("p j (n e) -> p e n j", e=PAIR),
+                    in1=inv_row[:]
+                    .rearrange("p (e n) -> p e n", e=PAIR)
+                    .unsqueeze(3)
+                    .to_broadcast([P, PAIR, GROUP // PAIR, PACK]),
                     op=ALU.mult,
                 )
+            live["grouped_x", s] = grouped_x
+
+        def quantise_x(s):
+            grouped_x = live.pop(("grouped_x", s))
+            x_words = work.tile([P, PASSES, GROUP], U32, name="x_words", align_bytes=64)
+            x_scales = work.tile([P, PASSES, GROUP], U8, name="x_scales", align_bytes=64)
             for g in range(PASSES):
-                nc.vector.quantize_mx(
-                    out=x_codes[:, g, :].bitcast(FP8X4),
-                    scales=x_scales[:, g, :],
-                    in_=grouped_x[:, g].rearrange("p n j -> p (n j)"),
-                )
-            live["x", s] = (x_codes, x_scales)
+                quantise(x_words[:, g, :], x_scales[:, g, :], grouped_x[:, g])
+            live["x", s] = (x_words, x_scales)
 
-        def hidden_layer(s):
-            x_codes, x_scales = live.pop(("x", s))
-            h_planes = work.tile([P, F_TILES, GROUP], BF16, name="h_planes")
-            for t in range(F_TILES):
-                f_cols = slice(t * P, (t + 1) * P)
-                h_acc = ps_h.tile([P, GROUP], F32, name="h_acc")
-                for g in range(PASSES):
-                    nc.tensor.matmul_mx(
-                        out=h_acc[:],
-                        lhsT=w1_codes[:, g, f_cols].bitcast(FP8X4),
-                        lhsT_scale=w1_scales[:, g, f_cols],
-                        rhs=x_codes[:, g, :].bitcast(FP8X4),
-                        rhs_scale=x_scales[:, g, :],
-                        start=(g == 0),
-                        stop=(g == PASSES - 1),
-                    )
-                nc.scalar.activation(
-                    out=h_planes[:, t, :], in_=h_acc[:], func=ACT.Relu, bias=b1_cols[:, t : t + 1]
+        def hidden(s, t):
+            if t == 0:
+                live["h_planes", s] = work.tile([P, F_TILES, GROUP], BF16, name="h_planes")
+            x_words, x_scales = live["x", s]
+            f_cols = slice(t * P, (t + 1) * P)
+            h_acc = ps_h.tile([P, GROUP], F32, name="h_acc")
+            for g in range(PASSES):
+                nc.tensor.matmul_mx(
+                    out=h_acc[:],
+                    lhsT=w1_words[:, g, f_cols].bitcast(FP8X4),
+                    lhsT_scale=w1_scales[:, g, f_cols],
+                    rhs=x_words[:, g, :].bitcast(FP8X4),
+                    rhs_scale=x_scales[:, g, :],
+                    start=(g == 0),
+                    stop=(g == PASSES - 1),
                 )
-            grouped_h = work.tile([P, GROUP, PACK], BF16, name="grouped_h", align_bytes=64)
-            nc.vector.tensor_copy(out=grouped_h[:], in_=h_planes[:].rearrange("p t n -> p n t"))
-            h_codes = codes.tile([P, GROUP], U32, name="h_codes", align_bytes=64)
-            h_scales = codes.tile([P, GROUP], U8, name="h_scales", align_bytes=64)
-            nc.vector.quantize_mx(
-                out=h_codes[:].bitcast(FP8X4),
-                scales=h_scales[:],
-                in_=grouped_h[:].rearrange("p n t -> p (n t)"),
+            nc.scalar.activation(
+                out=live["h_planes", s][:, t, :],
+                in_=h_acc[:],
+                func=ACT.Relu,
+                bias=b1_cols[:, t : t + 1],
             )
-            live["h", s] = (h_codes, h_scales)
 
-        def codes_and_statistics(s):
-            h_codes, h_scales = live.pop(("h", s))
+        def regroup_h(s):
+            grouped_h = work.tile([P, GROUP, PACK], BF16, name="grouped_h", align_bytes=64)
+            regroup(nc.vector.tensor_copy, grouped_h[:], live.pop(("h_planes", s))[:])
+            live["grouped_h", s] = grouped_h
+
+        def quantise_h(s):
+            h_words = work.tile([P, GROUP], U32, name="h_words", align_bytes=64)
+            h_scales = work.tile([P, GROUP], U8, name="h_scales", align_bytes=64)
+            quantise(h_words[:], h_scales[:], live.pop(("grouped_h", s))[:])
+            live["h", s] = (h_words, h_scales)
+
+        def project(s):
+            h_words, h_scales = live.pop(("h", s))
             z_acc = ps_z.tile([P, TILES, FEATURES], F32, name="z_acc")
             for i in range(TILES):
                 rows = slice(i * P, (i + 1) * P)
                 nc.tensor.matmul_mx(
                     out=z_acc[:, i, :],
-                    lhsT=h_codes[:, rows].bitcast(FP8X4),
+                    lhsT=h_words[:, rows].bitcast(FP8X4),
                     lhsT_scale=h_scales[:, rows],
-                    rhs=w2_codes[:].bitcast(FP8X4),
+                    rhs=w2_words[:].bitcast(FP8X4),
                     rhs_scale=w2_scales[:],
                     start=True,
                     stop=True,
                 )
-            zq = work.tile([P, TILES, FEATURES], F32, name="zq")
+            live["z_acc", s] = z_acc
+
+        def statistics(s):
+            zq = late.tile([P, TILES, FEATURES], F32, name="zq")
             nc.vector.tensor_tensor(
                 out=zq[:],
-                in0=z_acc[:],
+                in0=live.pop(("z_acc", s))[:],
                 in1=b2_f[:].unsqueeze(1).to_broadcast([P, TILES, FEATURES]),
                 op=ALU.add,
             )
@@ -221,56 +240,105 @@ def tile_spatialmemorymodule_pb_kernel(tc, z, Wq1, bq1, Wq2, bq2, out_0, out_1):
                 nc.vector.bn_stats(out=stats[:, i, :], in_=zq[:, i, :])
             for i in range(TILES):
                 nc.vector.bn_aggr(out=mean_var[:, i, :], in_=stats[:, i, :])
-            sum_sq = small.tile([P, TILES], F32, name="sum_sq")
-            nc.vector.tensor_scalar(
-                out=sum_sq[:],
-                in0=mean_var[:, :, 1],
-                scalar1=float(FEATURES),
-                scalar2=EPS_SQUARED,
-                op0=ALU.mult,
-                op1=ALU.max,
-            )
             nc.vector.tensor_scalar_mul(
-                out=var_all[:, s * TILES : (s + 1) * TILES],
-                in0=mean_var[:, :, 1],
+                out=var_all[:, :, s * BLOCKS : (s + 1) * BLOCKS],
+                in0=mean_var[:, :, 1].rearrange("p (e b) -> p e b", e=PAIR),
                 scalar1=FEATURES / (FEATURES - 1.0),
             )
+            live["zq", s] = (zq, mean_var)
+
+        def lengths(s):
             length = small.tile([P, TILES], F32, name="length")
-            nc.scalar.activation(out=length[:], in_=sum_sq[:], func=ACT.Sqrt)
+            clamped_root(length[:], live["zq", s][1][:, :, 1], float(FEATURES))
+            live["length", s] = length
+
+        def invert_lengths(s):
+            mean_var = live["zq", s][1]
             inv_length = small.tile([P, TILES], F32, name="inv_length")
-            nc.vector.reciprocal(out=inv_length[:], in_=length[:])
-            zc = work.tile([P, TILES, FEATURES], F32, name="zc")
+            nc.vector.reciprocal(out=inv_length[:], in_=live.pop(("length", s))[:])
+            shift = small.tile([P, TILES], F32, name="shift")
+            nc.vector.scalar_tensor_tensor(
+                out=shift[:],
+                in0=mean_var[:, :, 0],
+                scalar=-1.0,
+                in1=inv_length[:],
+                op0=ALU.mult,
+                op1=ALU.mult,
+            )
+            live["scale_shift", s] = (inv_length, shift)
+
+        def centre_and_store(s):
+            zq = live.pop(("zq", s))[0]
+            inv_length, shift = live.pop(("scale_shift", s))
+            zc = late.tile([P, BLOCKS, PAIR, FEATURES], F32, name="zc")
             for i in range(TILES):
-                nc.vector.tensor_scalar(
-                    out=zc[:, i, :],
-                    in0=zq[:, i, :],
-                    scalar1=mean_var[:, i, 0:1],
-                    scalar2=inv_length[:, i : i + 1],
-                    op0=ALU.subtract,
-                    op1=ALU.mult,
+                nc.scalar.activation(
+                    out=zc[:, i % BLOCKS, i // BLOCKS, :],
+                    in_=zq[:, i, :],
+                    func=ACT.Identity,
+                    scale=inv_length[:, i : i + 1],
+                    bias=shift[:, i : i + 1],
                 )
             nc.sync.dma_start(
-                out=out_0[s * GROUP : (s + 1) * GROUP, :].rearrange("(i p) d -> p i d", p=P),
-                in_=zc[:],
+                out=out_0[s * GROUP : (s + 1) * GROUP, :].rearrange(
+                    "(b p e) d -> p b (e d)", p=P, e=PAIR
+                ),
+                in_=zc[:].rearrange("p b e d -> p b (e d)"),
             )
 
-        stages = [
-            token_norms,
-            spread_inverse_norms,
-            normalise_and_quantise,
-            hidden_layer,
-            codes_and_statistics,
-        ]
-        for step in range(GROUPS + len(stages) - 1):
-            for lag, stage in enumerate(stages):
-                if 0 <= step - lag < GROUPS:
-                    stage(step - lag)
+        for q in range(AHEAD):
+            transposes(q)
 
-        var_t = ps_z.tile([P, P], F32, tag="z_acc")
-        nc.tensor.transpose(var_t[:], var_all[:], ident_f[:])
-        var_rows = const.tile([P, P], F32)
-        nc.vector.tensor_copy(out=var_rows[:], in_=var_t[:])
-        token_tiles = GROUPS * TILES
+        b2_f = const.tile([P, FEATURES], F32)
+        nc.vector.tensor_copy(out=b2_f[:], in_=b2_bf[:])
+        w2_grouped = const.tile([P, FEATURES, PACK], BF16, align_bytes=64)
+        regroup(nc.vector.tensor_copy, w2_grouped[:], w2_raw[:])
+        w1_grouped = work.tile([P, PASSES, HIDDEN, PACK], BF16, tag="grouped_x", align_bytes=64)
+        for g in range(PASSES):
+            regroup(nc.vector.tensor_copy, w1_grouped[:, g], w1_raw[:, g])
+        w2_words = const.tile([P, FEATURES], U32, align_bytes=64)
+        w2_scales = const.tile([P, FEATURES], U8, align_bytes=64)
+        quantise(w2_words[:], w2_scales[:], w2_grouped[:])
+        w1_words = const.tile([P, PASSES, HIDDEN], U32, align_bytes=64)
+        w1_scales = const.tile([P, PASSES, HIDDEN], U8, align_bytes=64)
+        for g in range(PASSES):
+            quantise(w1_words[:, g, :], w1_scales[:, g, :], w1_grouped[:, g])
+        b1_t = ps_z.tile([P, P], BF16, tag="z_acc")
+        nc.tensor.transpose(b1_t[:], b1_rows[:], ident_bf[:])
+        b1_cols = const.tile([P, F_TILES], F32)
+        nc.vector.tensor_copy(out=b1_cols[:], in_=b1_t[:, 0:F_TILES])
+
+        def at(stage, s, *more):
+            if 0 <= s < GROUPS:
+                stage(s, *more)
+
+        for i in range(GROUPS + DEEPEST_LAG + 1):
+            at(invert_norms, i - 1)
+            at(spread_inverse_norms, i - 1)
+            at(regroup_h, i - 3)
+            at(statistics, i - 4)
+            at(invert_lengths, i - 5)
+            at(quantise_h, i - 3)
+            at(normalise, i - 1)
+            at(quantise_x, i - 1)
+            for k in range(TILES):
+                if i < GROUPS:
+                    squares(i * TILES + k)
+                at(hidden, i - 2, k)
+                if i * TILES + k + AHEAD < GROUPS * TILES:
+                    transposes(i * TILES + k + AHEAD)
+            at(project, i - 3)
+            at(add_passes, i)
+            at(norms, i)
+            at(lengths, i - 4)
+            at(centre_and_store, i - 5)
+
+        var_t = ps_z.tile([P, PAIR, P], F32, tag="z_acc")
+        for e in range(PAIR):
+            nc.tensor.transpose(var_t[:, e, :], var_all[:, e, :], ident_f[:])
+        var_rows = const.tile([P, P, PAIR], F32)
+        nc.vector.tensor_copy(out=var_rows[:], in_=var_t[:].rearrange("c e p -> c p e"))
         nc.sync.dma_start(
-            out=out_1.rearrange("(c p) o -> c (p o)", p=P), in_=var_rows[0:token_tiles, :]
+            out=out_1.rearrange("(c p e) o -> c (p e o)", p=P, e=PAIR),
+            in_=var_rows[0 : GROUPS * BLOCKS].rearrange("c p e -> c (p e)"),
         )

@@ -23,8 +23,6 @@ GROUPS = BATCH * PIXELS // GROUP
 GROUPS_PER_IMAGE = PIXELS // GROUP
 EPS_SQUARED = 1e-24
 RUN = 4
-PAIR = 2
-BLOCKS = GROUP // (PAIR * P)
 AHEAD = 2
 DEEPEST_LAG = 5
 
@@ -87,7 +85,7 @@ def tile_spatialmemorymodule_pb_kernel(tc, z, Wq1, bq1, Wq2, bq2, out_0, out_1):
         make_identity(nc, ident_bf[:])
         ident_f = const.tile([P, P], F32)
         make_identity(nc, ident_f[:])
-        var_all = const.tile([P, PAIR, P], F32)
+        var_all = const.tile([P, P], F32)
         nc.vector.memset(var_all[:], 0.0)
         one = const.tile([P, 1], F32)
         nc.vector.memset(one[:], 1.0)
@@ -95,37 +93,26 @@ def tile_spatialmemorymodule_pb_kernel(tc, z, Wq1, bq1, Wq2, bq2, out_0, out_1):
 
         live = {}
 
-        def transposes(u):
-            s, b, g = u // TILES, u % TILES // PASSES, u % PASSES
-            words = x_all[s][:].bitcast(F32)
-            x_t = ps_t.tile([P, PACK, P], F32, name="x_t")
-            for j in range(PACK):
-                nc.tensor.transpose(x_t[:, j, :], words[:, g, j, b * P : (b + 1) * P], ident_f[:])
-            live["x_t", u] = x_t
+        def transposes(q):
+            x_sb = x_all[q // TILES]
+            cols = slice((q % TILES) * P, (q % TILES + 1) * P)
+            x_t = ps_t.tile([P, PASSES * PACK, P], BF16, name="x_t")
+            for g in range(PASSES):
+                for j in range(PACK):
+                    nc.tensor.transpose(x_t[:, g * PACK + j, :], x_sb[:, g, j, cols], ident_bf[:])
+            live["x_t", q] = x_t
 
-        def squares(u):
-            s, b, g = u // TILES, u % TILES // PASSES, u % PASSES
-            if u % TILES == 0:
-                live["norm_parts", s] = small.tile([P, PAIR, BLOCKS, PASSES], F32, name="norm_parts")
-            halves = live.pop(("x_t", u))[:].bitcast(BF16).rearrange("p j (k e) -> p e j k", e=PAIR)
-            for e in range(PAIR):
-                unused = work.tile([P, PACK, P], BF16, name="unused")
-                nc.scalar.activation(
-                    out=unused[:],
-                    in_=halves[:, e],
-                    func=ACT.Square,
-                    accum_out=live["norm_parts", s][:, e, b, g : g + 1],
-                )
-
-        def add_passes(s):
-            norm_sq = small.tile([P, TILES], F32, name="norm_sq")
-            nc.vector.tensor_reduce(
-                out=norm_sq[:],
-                in_=live.pop(("norm_parts", s))[:].rearrange("p e b g -> p (e b) g"),
-                axis=mybir.AxisListType.X,
-                op=ALU.add,
+        def squares(q):
+            if q % TILES == 0:
+                live["norm_sq", q // TILES] = small.tile([P, TILES], F32, name="norm_sq")
+            x_t = live.pop(("x_t", q))
+            unused = work.tile([P, CHANNELS], BF16, name="unused")
+            nc.scalar.activation(
+                out=unused[:],
+                in_=x_t[:].rearrange("p a k -> p (a k)"),
+                func=ACT.Square,
+                accum_out=live["norm_sq", q // TILES][:, q % TILES : q % TILES + 1],
             )
-            live["norm_sq", s] = norm_sq
 
         def clamped_root(out, in_, scale):
             above = small.tile([P, TILES], F32, name="above")
@@ -146,10 +133,12 @@ def tile_spatialmemorymodule_pb_kernel(tc, z, Wq1, bq1, Wq2, bq2, out_0, out_1):
             inv_norm = live.pop(("inv_norm", s))
             inv_row = ps_r.tile([P, GROUP], F32, name="inv_row")
             for i in range(TILES):
-                nc.tensor.transpose(
+                nc.tensor.matmul(
                     inv_row[:, i * P : (i + 1) * P],
-                    inv_norm[:, i : i + 1].to_broadcast([P, P]),
-                    ident_f[:],
+                    lhsT=inv_norm[:, i : i + 1].to_broadcast([P, P]),
+                    rhs=ident_f[:],
+                    start=True,
+                    stop=True,
                 )
             live["inv_row", s] = inv_row
 
@@ -158,12 +147,9 @@ def tile_spatialmemorymodule_pb_kernel(tc, z, Wq1, bq1, Wq2, bq2, out_0, out_1):
             grouped_x = work.tile([P, PASSES, GROUP, PACK], BF16, name="grouped_x", align_bytes=64)
             for g in range(PASSES):
                 nc.vector.tensor_tensor(
-                    out=grouped_x[:, g].rearrange("p (e n) j -> p e n j", e=PAIR),
-                    in0=x_all[s][:, g].rearrange("p j (n e) -> p e n j", e=PAIR),
-                    in1=inv_row[:]
-                    .rearrange("p (e n) -> p e n", e=PAIR)
-                    .unsqueeze(3)
-                    .to_broadcast([P, PAIR, GROUP // PAIR, PACK]),
+                    out=grouped_x[:, g],
+                    in0=x_all[s][:, g].rearrange("p j n -> p n j"),
+                    in1=inv_row[:].unsqueeze(2).to_broadcast([P, GROUP, PACK]),
                     op=ALU.mult,
                 )
             live["grouped_x", s] = grouped_x
@@ -241,8 +227,8 @@ def tile_spatialmemorymodule_pb_kernel(tc, z, Wq1, bq1, Wq2, bq2, out_0, out_1):
             for i in range(TILES):
                 nc.vector.bn_aggr(out=mean_var[:, i, :], in_=stats[:, i, :])
             nc.vector.tensor_scalar_mul(
-                out=var_all[:, :, s * BLOCKS : (s + 1) * BLOCKS],
-                in0=mean_var[:, :, 1].rearrange("p (e b) -> p e b", e=PAIR),
+                out=var_all[:, s * TILES : (s + 1) * TILES],
+                in0=mean_var[:, :, 1],
                 scalar1=FEATURES / (FEATURES - 1.0),
             )
             live["zq", s] = (zq, mean_var)
@@ -270,20 +256,18 @@ def tile_spatialmemorymodule_pb_kernel(tc, z, Wq1, bq1, Wq2, bq2, out_0, out_1):
         def centre_and_store(s):
             zq = live.pop(("zq", s))[0]
             inv_length, shift = live.pop(("scale_shift", s))
-            zc = late.tile([P, BLOCKS, PAIR, FEATURES], F32, name="zc")
+            zc = late.tile([P, TILES, FEATURES], F32, name="zc")
             for i in range(TILES):
                 nc.scalar.activation(
-                    out=zc[:, i % BLOCKS, i // BLOCKS, :],
+                    out=zc[:, i, :],
                     in_=zq[:, i, :],
                     func=ACT.Identity,
                     scale=inv_length[:, i : i + 1],
                     bias=shift[:, i : i + 1],
                 )
             nc.sync.dma_start(
-                out=out_0[s * GROUP : (s + 1) * GROUP, :].rearrange(
-                    "(b p e) d -> p b (e d)", p=P, e=PAIR
-                ),
-                in_=zc[:].rearrange("p b e d -> p b (e d)"),
+                out=out_0[s * GROUP : (s + 1) * GROUP, :].rearrange("(i p) d -> p i d", p=P),
+                in_=zc[:],
             )
 
         for q in range(AHEAD):
@@ -328,17 +312,14 @@ def tile_spatialmemorymodule_pb_kernel(tc, z, Wq1, bq1, Wq2, bq2, out_0, out_1):
                 if i * TILES + k + AHEAD < GROUPS * TILES:
                     transposes(i * TILES + k + AHEAD)
             at(project, i - 3)
-            at(add_passes, i)
             at(norms, i)
             at(lengths, i - 4)
             at(centre_and_store, i - 5)
 
-        var_t = ps_z.tile([P, PAIR, P], F32, tag="z_acc")
-        for e in range(PAIR):
-            nc.tensor.transpose(var_t[:, e, :], var_all[:, e, :], ident_f[:])
-        var_rows = const.tile([P, P, PAIR], F32)
-        nc.vector.tensor_copy(out=var_rows[:], in_=var_t[:].rearrange("c e p -> c p e"))
+        var_t = ps_z.tile([P, P], F32, tag="z_acc")
+        nc.tensor.transpose(var_t[:], var_all[:], ident_f[:])
+        var_rows = const.tile([P, P], F32)
+        nc.vector.tensor_copy(out=var_rows[:], in_=var_t[:])
         nc.sync.dma_start(
-            out=out_1.rearrange("(c p e) o -> c (p e o)", p=P, e=PAIR),
-            in_=var_rows[0 : GROUPS * BLOCKS].rearrange("c p e -> c (p e)"),
+            out=out_1.rearrange("(c p) o -> c (p o)", p=P), in_=var_rows[0 : GROUPS * TILES, :]
         )

@@ -24,7 +24,7 @@ GROUPS_PER_IMAGE = PIXELS // GROUP
 EPS_SQUARED = 1e-24
 RUN = 4
 AHEAD = 2
-DEEPEST_LAG = 5
+DEEPEST_LAG = 4
 
 FLOPS = 2 * BATCH * PIXELS * (CHANNELS * HIDDEN + HIDDEN * FEATURES)
 
@@ -87,9 +87,8 @@ def tile_spatialmemorymodule_pb_kernel(tc, z, Wq1, bq1, Wq2, bq2, out_0, out_1):
         make_identity(nc, ident_f[:])
         var_all = const.tile([P, P], F32)
         nc.vector.memset(var_all[:], 0.0)
-        one = const.tile([P, 1], F32)
-        nc.vector.memset(one[:], 1.0)
-        nc.scalar.activation(out=one[:], in_=one[:], func=ACT.Sqrt)
+        minus_half = const.tile([P, TILES], F32)
+        nc.vector.memset(minus_half[:], -0.5)
 
         live = {}
 
@@ -114,31 +113,26 @@ def tile_spatialmemorymodule_pb_kernel(tc, z, Wq1, bq1, Wq2, bq2, out_0, out_1):
                 accum_out=live["norm_sq", q // TILES][:, q % TILES : q % TILES + 1],
             )
 
-        def clamped_root(out, in_, scale):
-            above = small.tile([P, TILES], F32, name="above")
-            nc.scalar.activation(out=above[:], in_=in_, func=ACT.Relu, scale=scale, bias=-EPS_SQUARED)
-            nc.scalar.activation(out=out, in_=above[:], func=ACT.Sqrt, bias=EPS_SQUARED)
+        def inverse_root(out, in_, scale):
+            clamped = small.tile([P, TILES], F32, name="clamped")
+            nc.gpsimd.tensor_scalar(
+                out=clamped[:], in0=in_, scalar1=scale, scalar2=EPS_SQUARED, op0=ALU.mult, op1=ALU.max
+            )
+            nc.gpsimd.tensor_tensor(out=out, in0=clamped[:], in1=minus_half[:], op=ALU.pow)
 
-        def norms(s):
-            norm = small.tile([P, TILES], F32, name="norm")
-            clamped_root(norm[:], live.pop(("norm_sq", s))[:], 1.0)
-            live["norm", s] = norm
-
-        def invert_norms(s):
+        def inverse_norms(s):
             inv_norm = small.tile([P, TILES], F32, name="inv_norm")
-            nc.vector.reciprocal(out=inv_norm[:], in_=live.pop(("norm", s))[:])
+            inverse_root(inv_norm[:], live.pop(("norm_sq", s))[:], 1.0)
             live["inv_norm", s] = inv_norm
 
         def spread_inverse_norms(s):
             inv_norm = live.pop(("inv_norm", s))
             inv_row = ps_r.tile([P, GROUP], F32, name="inv_row")
             for i in range(TILES):
-                nc.tensor.matmul(
+                nc.tensor.transpose(
                     inv_row[:, i * P : (i + 1) * P],
-                    lhsT=inv_norm[:, i : i + 1].to_broadcast([P, P]),
-                    rhs=ident_f[:],
-                    start=True,
-                    stop=True,
+                    inv_norm[:, i : i + 1].to_broadcast([P, P]),
+                    ident_f[:],
                 )
             live["inv_row", s] = inv_row
 
@@ -226,44 +220,38 @@ def tile_spatialmemorymodule_pb_kernel(tc, z, Wq1, bq1, Wq2, bq2, out_0, out_1):
                 nc.vector.bn_stats(out=stats[:, i, :], in_=zq[:, i, :])
             for i in range(TILES):
                 nc.vector.bn_aggr(out=mean_var[:, i, :], in_=stats[:, i, :])
-            nc.vector.tensor_scalar_mul(
+            live["zq", s] = (zq, mean_var)
+
+        def centre_and_store(s):
+            zq, mean_var = live.pop(("zq", s))
+            nc.gpsimd.tensor_scalar(
                 out=var_all[:, s * TILES : (s + 1) * TILES],
                 in0=mean_var[:, :, 1],
                 scalar1=FEATURES / (FEATURES - 1.0),
-            )
-            live["zq", s] = (zq, mean_var)
-
-        def lengths(s):
-            length = small.tile([P, TILES], F32, name="length")
-            clamped_root(length[:], live["zq", s][1][:, :, 1], float(FEATURES))
-            live["length", s] = length
-
-        def invert_lengths(s):
-            mean_var = live["zq", s][1]
-            inv_length = small.tile([P, TILES], F32, name="inv_length")
-            nc.vector.reciprocal(out=inv_length[:], in_=live.pop(("length", s))[:])
-            shift = small.tile([P, TILES], F32, name="shift")
-            nc.vector.scalar_tensor_tensor(
-                out=shift[:],
-                in0=mean_var[:, :, 0],
-                scalar=-1.0,
-                in1=inv_length[:],
+                scalar2=0.0,
                 op0=ALU.mult,
-                op1=ALU.mult,
+                op1=ALU.add,
             )
-            live["scale_shift", s] = (inv_length, shift)
-
-        def centre_and_store(s):
-            zq = live.pop(("zq", s))[0]
-            inv_length, shift = live.pop(("scale_shift", s))
+            inv_length = small.tile([P, TILES], F32, name="inv_length")
+            inverse_root(inv_length[:], mean_var[:, :, 1], float(FEATURES))
+            minus_mean = small.tile([P, TILES], F32, name="minus_mean")
+            nc.gpsimd.tensor_scalar(
+                out=minus_mean[:],
+                in0=mean_var[:, :, 0],
+                scalar1=-1.0,
+                scalar2=0.0,
+                op0=ALU.mult,
+                op1=ALU.add,
+            )
             zc = late.tile([P, TILES, FEATURES], F32, name="zc")
             for i in range(TILES):
-                nc.scalar.activation(
+                nc.gpsimd.tensor_scalar(
                     out=zc[:, i, :],
-                    in_=zq[:, i, :],
-                    func=ACT.Identity,
-                    scale=inv_length[:, i : i + 1],
-                    bias=shift[:, i : i + 1],
+                    in0=zq[:, i, :],
+                    scalar1=minus_mean[:, i : i + 1],
+                    scalar2=inv_length[:, i : i + 1],
+                    op0=ALU.add,
+                    op1=ALU.mult,
                 )
             nc.sync.dma_start(
                 out=out_0[s * GROUP : (s + 1) * GROUP, :].rearrange("(i p) d -> p i d", p=P),
@@ -297,11 +285,9 @@ def tile_spatialmemorymodule_pb_kernel(tc, z, Wq1, bq1, Wq2, bq2, out_0, out_1):
                 stage(s, *more)
 
         for i in range(GROUPS + DEEPEST_LAG + 1):
-            at(invert_norms, i - 1)
             at(spread_inverse_norms, i - 1)
             at(regroup_h, i - 3)
             at(statistics, i - 4)
-            at(invert_lengths, i - 5)
             at(quantise_h, i - 3)
             at(normalise, i - 1)
             at(quantise_x, i - 1)
@@ -312,9 +298,8 @@ def tile_spatialmemorymodule_pb_kernel(tc, z, Wq1, bq1, Wq2, bq2, out_0, out_1):
                 if i * TILES + k + AHEAD < GROUPS * TILES:
                     transposes(i * TILES + k + AHEAD)
             at(project, i - 3)
-            at(norms, i)
-            at(lengths, i - 4)
-            at(centre_and_store, i - 5)
+            at(inverse_norms, i)
+            at(centre_and_store, i - 4)
 
         var_t = ps_z.tile([P, P], F32, tag="z_acc")
         nc.tensor.transpose(var_t[:], var_all[:], ident_f[:])

@@ -141,9 +141,12 @@ def tile_spatialmemorymodule_pb_kernel(tc, z, Wq1, bq1, Wq2, bq2, out_0, out_1):
             grouped_x = work.tile([P, PASSES, GROUP, PACK], BF16, name="grouped_x", align_bytes=64)
             for g in range(PASSES):
                 nc.vector.tensor_tensor(
-                    out=grouped_x[:, g],
-                    in0=x_all[s][:, g].rearrange("p j n -> p n j"),
-                    in1=inv_row[:].unsqueeze(2).to_broadcast([P, GROUP, PACK]),
+                    out=grouped_x[:, g].rearrange("p (c i) t -> p c t i", i=RUN),
+                    in0=x_all[s][:, g].rearrange("p t (c i) -> p c t i", i=RUN),
+                    in1=inv_row[:]
+                    .rearrange("p (c i) -> p c i", i=RUN)
+                    .unsqueeze(2)
+                    .to_broadcast([P, GROUP // RUN, PACK, RUN]),
                     op=ALU.mult,
                 )
             live["grouped_x", s] = grouped_x

@@ -23,6 +23,8 @@ GROUPS = BATCH * PIXELS // GROUP
 GROUPS_PER_IMAGE = PIXELS // GROUP
 EPS_SQUARED = 1e-24
 RUN = 4
+DIRECT, TURNED = 2, 2
+WORD_ROWS = 2
 AHEAD = 2
 DEEPEST_LAG = 4
 
@@ -33,13 +35,14 @@ def tile_spatialmemorymodule_pb_kernel(tc, z, Wq1, bq1, Wq2, bq2, out_0, out_1):
     nc = tc.nc
     with ExitStack() as ctx:
         const = ctx.enter_context(tc.tile_pool(name="const", bufs=1))
-        xpool = ctx.enter_context(tc.tile_pool(name="xpool", bufs=GROUPS))
+        xpool = ctx.enter_context(tc.tile_pool(name="xpool", bufs=BATCH + 1))
         work = ctx.enter_context(tc.tile_pool(name="work", bufs=2))
         late = ctx.enter_context(tc.tile_pool(name="late", bufs=3))
         small = ctx.enter_context(tc.tile_pool(name="small", bufs=4))
         ps_t = ctx.enter_context(tc.psum_pool(name="ps_t", bufs=3))
+        ps_b = ctx.enter_context(tc.psum_pool(name="ps_b", bufs=1))
         ps_r = ctx.enter_context(tc.psum_pool(name="ps_r", bufs=1))
-        ps_h = ctx.enter_context(tc.psum_pool(name="ps_h", bufs=3))
+        ps_h = ctx.enter_context(tc.psum_pool(name="ps_h", bufs=2))
         ps_z = ctx.enter_context(tc.psum_pool(name="ps_z", bufs=1))
 
         def regroup(engine_copy, dst, src):
@@ -53,21 +56,34 @@ def tile_spatialmemorymodule_pb_kernel(tc, z, Wq1, bq1, Wq2, bq2, out_0, out_1):
                 out=words.bitcast(FP8X4), scales=scales, in_=grouped.rearrange("p c t -> p (c t)")
             )
 
-        x_all = []
+        x_direct, x_turned = {}, {}
 
-        def load_group(s):
-            x_sb = xpool.tile([P, PASSES, PACK, GROUP], BF16, name="x_sb")
-            image = z[s // GROUPS_PER_IMAGE].rearrange(
-                "(g p j) h w -> p g j (h w)", g=PASSES, j=PACK
+        def load_groups(first, count):
+            image, y = divmod(first, GROUPS_PER_IMAGE)
+            xd = xpool.tile([P, PASSES, PACK, count * DIRECT * P], BF16, name="xd")
+            xt = xpool.tile([P, PASSES * PACK, count * TURNED * P], BF16, name="xt")
+            d0 = y * DIRECT * P
+            t0 = (GROUPS_PER_IMAGE * DIRECT + y * TURNED) * P
+            nc.sync.dma_start(
+                out=xt[:],
+                in_=z[image].rearrange("(a p) h w -> p a (h w)", p=P)[
+                    :, :, t0 : t0 + count * TURNED * P
+                ],
             )
-            first = (s % GROUPS_PER_IMAGE) * GROUP
             for g in range(PASSES):
-                nc.sync.dma_start(out=x_sb[:, g], in_=image[:, g, :, first : first + GROUP])
-            x_all.append(x_sb)
+                nc.sync.dma_start(
+                    out=xd[:, g],
+                    in_=z[image].rearrange("(g p j) h w -> p g j (h w)", g=PASSES, j=PACK)[
+                        :, g, :, d0 : d0 + count * DIRECT * P
+                    ],
+                )
+            for i in range(count):
+                x_direct[first + i] = xd[:, :, :, i * DIRECT * P : (i + 1) * DIRECT * P]
+                x_turned[first + i] = xt[:, :, i * TURNED * P : (i + 1) * TURNED * P]
 
         b1_rows = const.tile([P, P], BF16)
         nc.vector.memset(b1_rows[:], 0.0)
-        load_group(0)
+        load_groups(0, 1)
         nc.sync.dma_start(out=b1_rows[0:F_TILES, :], in_=bq1.rearrange("(t p) -> t p", p=P))
         b2_bf = const.tile([P, FEATURES], BF16)
         nc.sync.dma_start(out=b2_bf[:], in_=bq2.partition_broadcast(P))
@@ -78,39 +94,66 @@ def tile_spatialmemorymodule_pb_kernel(tc, z, Wq1, bq1, Wq2, bq2, out_0, out_1):
             out=w1_raw[:].rearrange("p g j f -> p g (j f)"),
             in_=Wq1.rearrange("(g p j) f -> p g (j f)", g=PASSES, j=PACK),
         )
-        for s in range(1, GROUPS):
-            load_group(s)
+        load_groups(1, 1)
+        for s in range(GROUPS_PER_IMAGE, GROUPS, GROUPS_PER_IMAGE):
+            load_groups(s, GROUPS_PER_IMAGE)
 
         ident_bf = const.tile([P, P], BF16)
         make_identity(nc, ident_bf[:])
+        pairs_bf = const.tile([P, P], BF16)
+        nc.gpsimd.tensor_copy(
+            out=pairs_bf[:].rearrange("k (u p e) -> k p u e", u=WORD_ROWS, e=2),
+            in_=ident_bf[:].rearrange("k (p u e) -> k p u e", u=WORD_ROWS, e=2),
+        )
         ident_f = const.tile([P, P], F32)
         make_identity(nc, ident_f[:])
+        moments = const.tile([P, GROUPS * TILES, 2], F32)
         var_all = const.tile([P, P], F32)
         nc.vector.memset(var_all[:], 0.0)
         minus_half = const.tile([P, TILES], F32)
         nc.vector.memset(minus_half[:], -0.5)
+        table_call = const.tile([P, 1], F32)
+        nc.scalar.activation(
+            out=table_call[:], in_=minus_half[:, 0:1], func=ACT.Abs_reciprocal_sqrt
+        )
 
         live = {}
 
+        order = list(range(DIRECT, TILES)) + list(range(DIRECT))
+
         def transposes(q):
-            x_sb = x_all[q // TILES]
-            cols = slice((q % TILES) * P, (q % TILES + 1) * P)
-            x_t = ps_t.tile([P, PASSES * PACK, P], BF16, name="x_t")
+            s, k = q // TILES, order[q % TILES]
+            x_t = ps_t.tile([P, PASSES, WORD_ROWS, PACK, P // 2], BF16, name="x_t")
             for g in range(PASSES):
                 for j in range(PACK):
-                    nc.tensor.transpose(x_t[:, g * PACK + j, :], x_sb[:, g, j, cols], ident_bf[:])
-            live["x_t", q] = x_t
+                    if k < DIRECT:
+                        nc.tensor.transpose(
+                            x_t[:].rearrange("p g u b c -> p (g u b c)")[
+                                :, (g * PACK + j) * P : (g * PACK + j + 1) * P
+                            ],
+                            x_direct[s][:, g, j, k * P : (k + 1) * P],
+                            ident_bf[:],
+                        )
+                    else:
+                        nc.tensor.transpose(
+                            x_t[:, g, :, j, :],
+                            x_turned[s][:, g * PACK + j, (k - DIRECT) * P : (k - DIRECT + 1) * P],
+                            pairs_bf[:],
+                        )
+            live["x_t", s, k] = x_t
 
         def squares(q):
+            s, k = q // TILES, order[q % TILES]
             if q % TILES == 0:
-                live["norm_sq", q // TILES] = small.tile([P, TILES], F32, name="norm_sq")
-            x_t = live.pop(("x_t", q))
+                live["norm_sq", s] = small.tile([P, TILES], F32, name="norm_sq")
+                live["inv_norm", s] = small.tile([P, TILES], F32, name="inv_norm")
+            x_t = live["x_t", s, k]
             unused = work.tile([P, CHANNELS], BF16, name="unused")
             nc.scalar.activation(
                 out=unused[:],
-                in_=x_t[:].rearrange("p a k -> p (a k)"),
+                in_=x_t[:].rearrange("p g u b c -> p (g u b c)"),
                 func=ACT.Square,
-                accum_out=live["norm_sq", q // TILES][:, q % TILES : q % TILES + 1],
+                accum_out=live["norm_sq", s][:, k : k + 1],
             )
 
         def inverse_root(out, in_, scale):
@@ -120,15 +163,53 @@ def tile_spatialmemorymodule_pb_kernel(tc, z, Wq1, bq1, Wq2, bq2, out_0, out_1):
             )
             nc.gpsimd.tensor_tensor(out=out, in0=clamped[:], in1=minus_half[:], op=ALU.pow)
 
-        def inverse_norms(s):
-            inv_norm = small.tile([P, TILES], F32, name="inv_norm")
-            inverse_root(inv_norm[:], live.pop(("norm_sq", s))[:], 1.0)
-            live["inv_norm", s] = inv_norm
+        def inverse_norms(s, first, last):
+            clamped_norm = small.tile([P, TILES], F32, name="clamped_norm")
+            nc.vector.tensor_scalar(
+                out=clamped_norm[:, first:last],
+                in0=live["norm_sq", s][:, first:last],
+                scalar1=EPS_SQUARED,
+                scalar2=None,
+                op0=ALU.max,
+            )
+            nc.scalar.activation(
+                out=live["inv_norm", s][:, first:last],
+                in_=clamped_norm[:, first:last],
+                func=ACT.Abs_reciprocal_sqrt,
+            )
+
+        def grouped_tile(s):
+            if ("grouped_x", s) not in live:
+                live["grouped_x", s] = work.tile(
+                    [P, PASSES, GROUP, PACK], BF16, name="grouped_x", align_bytes=64
+                )
+            return live["grouped_x", s]
+
+        def scale_turned(s, k):
+            x_t = live.pop(("x_t", s, k))
+            xn = work.tile([P, PASSES, WORD_ROWS, 2 * P], BF16, name="xn")
+            nc.vector.tensor_scalar(
+                out=xn[:].rearrange("p g u c -> p (g u c)"),
+                in0=x_t[:].rearrange("p g u b c -> p (g u b c)"),
+                scalar1=live["inv_norm", s][:, k : k + 1],
+                scalar2=None,
+                op0=ALU.mult,
+            )
+            live["xn", s, k] = xn
+
+        def turn_back(s, k):
+            xn = live.pop(("xn", s, k))
+            x_b = ps_b.tile([P, PASSES, WORD_ROWS, P], F32, name="x_b")
+            for g in range(PASSES):
+                for u in range(WORD_ROWS):
+                    nc.tensor.transpose(x_b[:, g, u, :], xn[:, g, u, :].bitcast(F32), ident_f[:])
+            words = grouped_tile(s)[:, :, k * P : (k + 1) * P, :].bitcast(F32)
+            nc.scalar.copy(out=words, in_=x_b[:].rearrange("p g u n -> p g n u"))
 
         def spread_inverse_norms(s):
-            inv_norm = live.pop(("inv_norm", s))
-            inv_row = ps_r.tile([P, GROUP], F32, name="inv_row")
-            for i in range(TILES):
+            inv_norm = live["inv_norm", s]
+            inv_row = ps_r.tile([P, DIRECT * P], F32, name="inv_row")
+            for i in range(DIRECT):
                 nc.tensor.transpose(
                     inv_row[:, i * P : (i + 1) * P],
                     inv_norm[:, i : i + 1].to_broadcast([P, P]),
@@ -138,18 +219,17 @@ def tile_spatialmemorymodule_pb_kernel(tc, z, Wq1, bq1, Wq2, bq2, out_0, out_1):
 
         def normalise(s):
             inv_row = live.pop(("inv_row", s))
-            grouped_x = work.tile([P, PASSES, GROUP, PACK], BF16, name="grouped_x", align_bytes=64)
+            grouped_x = grouped_tile(s)
             for g in range(PASSES):
                 nc.vector.tensor_tensor(
-                    out=grouped_x[:, g].rearrange("p (c i) t -> p c t i", i=RUN),
-                    in0=x_all[s][:, g].rearrange("p t (c i) -> p c t i", i=RUN),
+                    out=grouped_x[:, g, 0 : DIRECT * P].rearrange("p (c i) t -> p c t i", i=RUN),
+                    in0=x_direct[s][:, g].rearrange("p t (c i) -> p c t i", i=RUN),
                     in1=inv_row[:]
                     .rearrange("p (c i) -> p c i", i=RUN)
                     .unsqueeze(2)
-                    .to_broadcast([P, GROUP // RUN, PACK, RUN]),
+                    .to_broadcast([P, DIRECT * P // RUN, PACK, RUN]),
                     op=ALU.mult,
                 )
-            live["grouped_x", s] = grouped_x
 
         def quantise_x(s):
             grouped_x = live.pop(("grouped_x", s))
@@ -218,23 +298,15 @@ def tile_spatialmemorymodule_pb_kernel(tc, z, Wq1, bq1, Wq2, bq2, out_0, out_1):
                 op=ALU.add,
             )
             stats = small.tile([P, TILES, 6], F32, name="stats")
-            mean_var = small.tile([P, TILES, 2], F32, name="mean_var")
             for i in range(TILES):
                 nc.vector.bn_stats(out=stats[:, i, :], in_=zq[:, i, :])
+            mean_var = moments[:, s * TILES : (s + 1) * TILES, :]
             for i in range(TILES):
                 nc.vector.bn_aggr(out=mean_var[:, i, :], in_=stats[:, i, :])
             live["zq", s] = (zq, mean_var)
 
         def centre_and_store(s):
             zq, mean_var = live.pop(("zq", s))
-            nc.gpsimd.tensor_scalar(
-                out=var_all[:, s * TILES : (s + 1) * TILES],
-                in0=mean_var[:, :, 1],
-                scalar1=FEATURES / (FEATURES - 1.0),
-                scalar2=0.0,
-                op0=ALU.mult,
-                op1=ALU.add,
-            )
             inv_length = small.tile([P, TILES], F32, name="inv_length")
             inverse_root(inv_length[:], mean_var[:, :, 1], float(FEATURES))
             minus_mean = small.tile([P, TILES], F32, name="minus_mean")
@@ -256,10 +328,14 @@ def tile_spatialmemorymodule_pb_kernel(tc, z, Wq1, bq1, Wq2, bq2, out_0, out_1):
                     op0=ALU.add,
                     op1=ALU.mult,
                 )
-            nc.sync.dma_start(
-                out=out_0[s * GROUP : (s + 1) * GROUP, :].rearrange("(i p) d -> p i d", p=P),
-                in_=zc[:],
-            )
+            image, y = divmod(s, GROUPS_PER_IMAGE)
+            tile_0 = image * GROUPS_PER_IMAGE * TILES + y * DIRECT
+            tile_1 = image * GROUPS_PER_IMAGE * TILES + GROUPS_PER_IMAGE * DIRECT + y * TURNED
+            for tile, k, count in ((tile_0, 0, DIRECT), (tile_1, DIRECT, TURNED)):
+                nc.sync.dma_start(
+                    out=out_0[tile * P : (tile + count) * P, :].rearrange("(i p) d -> p i d", p=P),
+                    in_=zc[:, k : k + count],
+                )
 
         for q in range(AHEAD):
             transposes(q)
@@ -297,13 +373,35 @@ def tile_spatialmemorymodule_pb_kernel(tc, z, Wq1, bq1, Wq2, bq2, out_0, out_1):
             for k in range(TILES):
                 if i < GROUPS:
                     squares(i * TILES + k)
+                    if k == TURNED - 1:
+                        inverse_norms(i, DIRECT, TILES)
+                        for t in range(DIRECT, TILES):
+                            scale_turned(i, t)
                 at(hidden, i - 2, k)
                 if i * TILES + k + AHEAD < GROUPS * TILES:
                     transposes(i * TILES + k + AHEAD)
+                if i < GROUPS and k >= TURNED:
+                    turn_back(i, k - TURNED + DIRECT)
+            if i < GROUPS:
+                for k in range(DIRECT):
+                    live.pop(("x_t", i, k))
+                inverse_norms(i, 0, DIRECT)
             at(project, i - 3)
-            at(inverse_norms, i)
             at(centre_and_store, i - 4)
 
+        for y in range(GROUPS_PER_IMAGE):
+            for first, count, place in ((0, DIRECT, y * DIRECT), (DIRECT, TURNED, GROUPS_PER_IMAGE * DIRECT + y * TURNED)):
+                nc.vector.tensor_scalar(
+                    out=var_all[:, 0 : GROUPS * TILES].rearrange("p (b k) -> p b k", b=BATCH)[
+                        :, :, place : place + count
+                    ],
+                    in0=moments[:].rearrange("p (b y k) m -> p y b k m", b=BATCH, y=GROUPS_PER_IMAGE)[
+                        :, y, :, first : first + count, 1
+                    ],
+                    scalar1=FEATURES / (FEATURES - 1.0),
+                    scalar2=None,
+                    op0=ALU.mult,
+                )
         var_t = ps_z.tile([P, P], F32, tag="z_acc")
         nc.tensor.transpose(var_t[:], var_all[:], ident_f[:])
         var_rows = const.tile([P, P], F32)

@@ -21,9 +21,10 @@ GROUP = 512
 TILES = GROUP // P
 GROUPS = BATCH * PIXELS // GROUP
 GROUPS_PER_IMAGE = PIXELS // GROUP
-EPS_SQUARED = 1e-24
+EPS = 1e-12
+TINY = 1e-30
 RUN = 4
-DIRECT, TURNED = 2, 2
+DIRECT, TURNED = 1, 3
 WORD_ROWS = 2
 AHEAD = 2
 DEEPEST_LAG = 4
@@ -110,12 +111,14 @@ def tile_spatialmemorymodule_pb_kernel(tc, z, Wq1, bq1, Wq2, bq2, out_0, out_1):
         moments = const.tile([P, GROUPS * TILES, 2], F32)
         var_all = const.tile([P, P], F32)
         nc.vector.memset(var_all[:], 0.0)
-        minus_half = const.tile([P, TILES], F32)
-        nc.vector.memset(minus_half[:], -0.5)
-        table_call = const.tile([P, 1], F32)
-        nc.scalar.activation(
-            out=table_call[:], in_=minus_half[:, 0:1], func=ACT.Abs_reciprocal_sqrt
+        one_col = const.tile([P, 1], F32)
+        nc.vector.memset(one_col[:], 1.0)
+        tiny = const.tile([P, 1], F32)
+        nc.vector.tensor_scalar(
+            out=tiny[:], in0=one_col[:], scalar1=TINY, scalar2=None, op0=ALU.mult
         )
+        table_call = const.tile([P, 1], F32)
+        nc.scalar.activation(out=table_call[:], in_=one_col[:], func=ACT.Abs_reciprocal_sqrt)
 
         live = {}
 
@@ -123,23 +126,28 @@ def tile_spatialmemorymodule_pb_kernel(tc, z, Wq1, bq1, Wq2, bq2, out_0, out_1):
 
         def transposes(q):
             s, k = q // TILES, order[q % TILES]
+            if k < DIRECT:
+                gram = ps_r.tile([P, P], F32, tag="inv_row", name="gram")
+                cols = slice(k * P, (k + 1) * P)
+                for g in range(PASSES):
+                    for j in range(PACK):
+                        nc.tensor.matmul(
+                            gram[:],
+                            lhsT=x_direct[s][:, g, j, cols],
+                            rhs=x_direct[s][:, g, j, cols],
+                            start=(g == 0 and j == 0),
+                            stop=(g == PASSES - 1 and j == PACK - 1),
+                        )
+                live["x_t", s, k] = gram
+                return
             x_t = ps_t.tile([P, PASSES, WORD_ROWS, PACK, P // 2], BF16, name="x_t")
             for g in range(PASSES):
                 for j in range(PACK):
-                    if k < DIRECT:
-                        nc.tensor.transpose(
-                            x_t[:].rearrange("p g u b c -> p (g u b c)")[
-                                :, (g * PACK + j) * P : (g * PACK + j + 1) * P
-                            ],
-                            x_direct[s][:, g, j, k * P : (k + 1) * P],
-                            ident_bf[:],
-                        )
-                    else:
-                        nc.tensor.transpose(
-                            x_t[:, g, :, j, :],
-                            x_turned[s][:, g * PACK + j, (k - DIRECT) * P : (k - DIRECT + 1) * P],
-                            pairs_bf[:],
-                        )
+                    nc.tensor.transpose(
+                        x_t[:, g, :, j, :],
+                        x_turned[s][:, g * PACK + j, (k - DIRECT) * P : (k - DIRECT + 1) * P],
+                        pairs_bf[:],
+                    )
             live["x_t", s, k] = x_t
 
         def squares(q):
@@ -147,6 +155,18 @@ def tile_spatialmemorymodule_pb_kernel(tc, z, Wq1, bq1, Wq2, bq2, out_0, out_1):
             if q % TILES == 0:
                 live["norm_sq", s] = small.tile([P, TILES], F32, name="norm_sq")
                 live["inv_norm", s] = small.tile([P, TILES], F32, name="inv_norm")
+            if k < DIRECT:
+                masked = work.tile([P, P], F32, name="masked")
+                nc.vector.scalar_tensor_tensor(
+                    out=masked[:],
+                    in0=live.pop(("x_t", s, k))[:],
+                    scalar=1.0,
+                    in1=ident_f[:],
+                    op0=ALU.mult,
+                    op1=ALU.mult,
+                    accum_out=live["norm_sq", s][:, k : k + 1],
+                )
+                return
             x_t = live["x_t", s, k]
             unused = work.tile([P, CHANNELS], BF16, name="unused")
             nc.scalar.activation(
@@ -156,27 +176,22 @@ def tile_spatialmemorymodule_pb_kernel(tc, z, Wq1, bq1, Wq2, bq2, out_0, out_1):
                 accum_out=live["norm_sq", s][:, k : k + 1],
             )
 
-        def inverse_root(out, in_, scale):
-            clamped = small.tile([P, TILES], F32, name="clamped")
-            nc.gpsimd.tensor_scalar(
-                out=clamped[:], in0=in_, scalar1=scale, scalar2=EPS_SQUARED, op0=ALU.mult, op1=ALU.max
-            )
-            nc.gpsimd.tensor_tensor(out=out, in0=clamped[:], in1=minus_half[:], op=ALU.pow)
-
-        def inverse_norms(s, first, last):
-            clamped_norm = small.tile([P, TILES], F32, name="clamped_norm")
-            nc.vector.tensor_scalar(
-                out=clamped_norm[:, first:last],
-                in0=live["norm_sq", s][:, first:last],
-                scalar1=EPS_SQUARED,
-                scalar2=None,
-                op0=ALU.max,
-            )
+        def inverse_root(out, in_, scale, width):
+            inverse = small.tile([P, TILES], F32, name="inverse")
             nc.scalar.activation(
-                out=live["inv_norm", s][:, first:last],
-                in_=clamped_norm[:, first:last],
+                out=inverse[:, 0:width],
+                in_=in_,
                 func=ACT.Abs_reciprocal_sqrt,
+                scale=scale,
+                bias=tiny[:],
             )
+            nc.vector.tensor_scalar(
+                out=out, in0=inverse[:, 0:width], scalar1=1.0 / EPS, scalar2=None, op0=ALU.min
+            )
+
+        def inverse_norm(s, k):
+            one = slice(k, k + 1)
+            inverse_root(live["inv_norm", s][:, one], live["norm_sq", s][:, one], 1.0, 1)
 
         def grouped_tile(s):
             if ("grouped_x", s) not in live:
@@ -308,7 +323,7 @@ def tile_spatialmemorymodule_pb_kernel(tc, z, Wq1, bq1, Wq2, bq2, out_0, out_1):
         def centre_and_store(s):
             zq, mean_var = live.pop(("zq", s))
             inv_length = small.tile([P, TILES], F32, name="inv_length")
-            inverse_root(inv_length[:], mean_var[:, :, 1], float(FEATURES))
+            inverse_root(inv_length[:], mean_var[:, :, 1], float(FEATURES), TILES)
             minus_mean = small.tile([P, TILES], F32, name="minus_mean")
             nc.gpsimd.tensor_scalar(
                 out=minus_mean[:],
@@ -370,22 +385,18 @@ def tile_spatialmemorymodule_pb_kernel(tc, z, Wq1, bq1, Wq2, bq2, out_0, out_1):
             at(quantise_h, i - 3)
             at(normalise, i - 1)
             at(quantise_x, i - 1)
-            for k in range(TILES):
+            for n in range(TILES):
                 if i < GROUPS:
-                    squares(i * TILES + k)
-                    if k == TURNED - 1:
-                        inverse_norms(i, DIRECT, TILES)
-                        for t in range(DIRECT, TILES):
-                            scale_turned(i, t)
-                at(hidden, i - 2, k)
-                if i * TILES + k + AHEAD < GROUPS * TILES:
-                    transposes(i * TILES + k + AHEAD)
-                if i < GROUPS and k >= TURNED:
-                    turn_back(i, k - TURNED + DIRECT)
-            if i < GROUPS:
-                for k in range(DIRECT):
-                    live.pop(("x_t", i, k))
-                inverse_norms(i, 0, DIRECT)
+                    k = order[n]
+                    squares(i * TILES + n)
+                    inverse_norm(i, k)
+                    if k >= DIRECT:
+                        scale_turned(i, k)
+                at(hidden, i - 2, n)
+                if i * TILES + n + AHEAD < GROUPS * TILES:
+                    transposes(i * TILES + n + AHEAD)
+                if i < GROUPS and 1 <= n <= TURNED:
+                    turn_back(i, order[n - 1])
             at(project, i - 3)
             at(centre_and_store, i - 4)
 

@@ -23,6 +23,7 @@ GROUPS = BATCH * PIXELS // GROUP
 GROUPS_PER_IMAGE = PIXELS // GROUP
 EPS = 1e-12
 TINY = 1e-30
+B2_ROW = 32
 RUN = 4
 DIRECT, TURNED = 1, 3
 WORD_ROWS = 2
@@ -36,7 +37,7 @@ def tile_spatialmemorymodule_pb_kernel(tc, z, Wq1, bq1, Wq2, bq2, out_0, out_1):
     nc = tc.nc
     with ExitStack() as ctx:
         const = ctx.enter_context(tc.tile_pool(name="const", bufs=1))
-        xpool = ctx.enter_context(tc.tile_pool(name="xpool", bufs=BATCH + 1))
+        xpool = ctx.enter_context(tc.tile_pool(name="xpool", bufs=BATCH))
         work = ctx.enter_context(tc.tile_pool(name="work", bufs=2))
         late = ctx.enter_context(tc.tile_pool(name="late", bufs=3))
         small = ctx.enter_context(tc.tile_pool(name="small", bufs=4))
@@ -59,45 +60,54 @@ def tile_spatialmemorymodule_pb_kernel(tc, z, Wq1, bq1, Wq2, bq2, out_0, out_1):
 
         x_direct, x_turned = {}, {}
 
-        def load_groups(first, count):
-            image, y = divmod(first, GROUPS_PER_IMAGE)
-            xd = xpool.tile([P, PASSES, PACK, count * DIRECT * P], BF16, name="xd")
-            xt = xpool.tile([P, PASSES * PACK, count * TURNED * P], BF16, name="xt")
-            d0 = y * DIRECT * P
-            t0 = (GROUPS_PER_IMAGE * DIRECT + y * TURNED) * P
-            nc.sync.dma_start(
-                out=xt[:],
-                in_=z[image].rearrange("(a p) h w -> p a (h w)", p=P)[
-                    :, :, t0 : t0 + count * TURNED * P
-                ],
-            )
-            for g in range(PASSES):
+        def load_image(image, pieces):
+            split = GROUPS_PER_IMAGE * DIRECT * P
+            xt = xpool.tile([P, PASSES * PACK, PIXELS - split], BF16, name="xt")
+            xd = xpool.tile([P, PASSES, PACK, split], BF16, name="xd")
+            from_turned = z[image].rearrange("(a p) h w -> p a (h w)", p=P)[:, :, split:]
+            from_direct = z[image].rearrange("(g p j) h w -> p g j (h w)", g=PASSES, j=PACK)
+            d, t = split // pieces, (PIXELS - split) // pieces
+            for i in range(pieces):
                 nc.sync.dma_start(
-                    out=xd[:, g],
-                    in_=z[image].rearrange("(g p j) h w -> p g j (h w)", g=PASSES, j=PACK)[
-                        :, g, :, d0 : d0 + count * DIRECT * P
-                    ],
+                    out=xt[:, :, i * t : (i + 1) * t], in_=from_turned[:, :, i * t : (i + 1) * t]
                 )
-            for i in range(count):
-                x_direct[first + i] = xd[:, :, :, i * DIRECT * P : (i + 1) * DIRECT * P]
-                x_turned[first + i] = xt[:, :, i * TURNED * P : (i + 1) * TURNED * P]
+                for g in range(PASSES):
+                    nc.sync.dma_start(
+                        out=xd[:, g, :, i * d : (i + 1) * d],
+                        in_=from_direct[:, g, :, i * d : (i + 1) * d],
+                    )
+                if image == 0:
+                    (load_biases, load_weights)[i]()
+            for y in range(GROUPS_PER_IMAGE):
+                x_turned[image * GROUPS_PER_IMAGE + y] = xt[:, :, y * TURNED * P : (y + 1) * TURNED * P]
+                x_direct[image * GROUPS_PER_IMAGE + y] = xd[:, :, :, y * DIRECT * P : (y + 1) * DIRECT * P]
 
-        b1_rows = const.tile([P, P], BF16)
-        nc.vector.memset(b1_rows[:], 0.0)
-        load_groups(0, 1)
-        nc.sync.dma_start(out=b1_rows[0:F_TILES, :], in_=bq1.rearrange("(t p) -> t p", p=P))
-        b2_bf = const.tile([P, FEATURES], BF16)
-        nc.sync.dma_start(out=b2_bf[:], in_=bq2.partition_broadcast(P))
+        bias_rows = const.tile([P, P], BF16)
+        nc.vector.memset(bias_rows[:], 0.0)
+        b2_select = const.tile([P, P], BF16)
+        nc.vector.memset(b2_select[:], 0.0)
+        nc.vector.memset(b2_select[B2_ROW : B2_ROW + 1, :], 1.0)
         w2_raw = const.tile([P, PACK, FEATURES], BF16)
-        nc.sync.dma_start(out=w2_raw[:], in_=Wq2.rearrange("(t p) d -> p t d", p=P))
-        w1_raw = work.tile([P, PASSES, PACK, HIDDEN], BF16, tag="grouped_x", align_bytes=64)
-        nc.sync.dma_start(
-            out=w1_raw[:].rearrange("p g j f -> p g (j f)"),
-            in_=Wq1.rearrange("(g p j) f -> p g (j f)", g=PASSES, j=PACK),
-        )
-        load_groups(1, 1)
-        for s in range(GROUPS_PER_IMAGE, GROUPS, GROUPS_PER_IMAGE):
-            load_groups(s, GROUPS_PER_IMAGE)
+        w1_raw = const.tile([P, PASSES, PACK, HIDDEN], BF16)
+
+        def load_biases():
+            nc.sync.dma_start(
+                out=bias_rows[0:F_TILES, :], in_=bq1.rearrange("(t p) -> t p", p=P)
+            )
+            nc.sync.dma_start(
+                out=bias_rows[B2_ROW : B2_ROW + 1, :], in_=bq2.rearrange("(o d) -> o d", o=1)
+            )
+
+        def load_weights():
+            nc.sync.dma_start(out=w2_raw[:], in_=Wq2.rearrange("(t p) d -> p t d", p=P))
+            nc.sync.dma_start(
+                out=w1_raw[:].rearrange("p g j f -> p g (j f)"),
+                in_=Wq1.rearrange("(g p j) f -> p g (j f)", g=PASSES, j=PACK),
+            )
+
+        load_image(0, GROUPS_PER_IMAGE)
+        for image in range(1, BATCH):
+            load_image(image, 1)
 
         ident_bf = const.tile([P, P], BF16)
         make_identity(nc, ident_bf[:])
@@ -324,8 +334,9 @@ def tile_spatialmemorymodule_pb_kernel(tc, z, Wq1, bq1, Wq2, bq2, out_0, out_1):
             zq, mean_var = live.pop(("zq", s))
             inv_length = small.tile([P, TILES], F32, name="inv_length")
             inverse_root(inv_length[:], mean_var[:, :, 1], float(FEATURES), TILES)
+            engine = nc.vector if s == GROUPS - 1 else nc.gpsimd
             minus_mean = small.tile([P, TILES], F32, name="minus_mean")
-            nc.gpsimd.tensor_scalar(
+            engine.tensor_scalar(
                 out=minus_mean[:],
                 in0=mean_var[:, :, 0],
                 scalar1=-1.0,
@@ -335,7 +346,7 @@ def tile_spatialmemorymodule_pb_kernel(tc, z, Wq1, bq1, Wq2, bq2, out_0, out_1):
             )
             zc = late.tile([P, TILES, FEATURES], F32, name="zc")
             for i in range(TILES):
-                nc.gpsimd.tensor_scalar(
+                engine.tensor_scalar(
                     out=zc[:, i, :],
                     in0=zq[:, i, :],
                     scalar1=minus_mean[:, i : i + 1],
@@ -356,23 +367,29 @@ def tile_spatialmemorymodule_pb_kernel(tc, z, Wq1, bq1, Wq2, bq2, out_0, out_1):
             transposes(q)
 
         b2_f = const.tile([P, FEATURES], F32)
-        nc.vector.tensor_copy(out=b2_f[:], in_=b2_bf[:])
         w2_grouped = const.tile([P, FEATURES, PACK], BF16, align_bytes=64)
-        regroup(nc.vector.tensor_copy, w2_grouped[:], w2_raw[:])
-        w1_grouped = work.tile([P, PASSES, HIDDEN, PACK], BF16, tag="grouped_x", align_bytes=64)
-        for g in range(PASSES):
-            regroup(nc.vector.tensor_copy, w1_grouped[:, g], w1_raw[:, g])
+        w1_grouped = const.tile([P, PASSES, HIDDEN, PACK], BF16, align_bytes=64)
         w2_words = const.tile([P, FEATURES], U32, align_bytes=64)
         w2_scales = const.tile([P, FEATURES], U8, align_bytes=64)
-        quantise(w2_words[:], w2_scales[:], w2_grouped[:])
         w1_words = const.tile([P, PASSES, HIDDEN], U32, align_bytes=64)
         w1_scales = const.tile([P, PASSES, HIDDEN], U8, align_bytes=64)
-        for g in range(PASSES):
-            quantise(w1_words[:, g, :], w1_scales[:, g, :], w1_grouped[:, g])
-        b1_t = ps_z.tile([P, P], BF16, tag="z_acc")
-        nc.tensor.transpose(b1_t[:], b1_rows[:], ident_bf[:])
         b1_cols = const.tile([P, F_TILES], F32)
-        nc.vector.tensor_copy(out=b1_cols[:], in_=b1_t[:, 0:F_TILES])
+
+        def regroup_weights(g):
+            regroup(nc.vector.tensor_copy, w1_grouped[:, g], w1_raw[:, g])
+
+        def quantise_weights(g):
+            quantise(w1_words[:, g, :], w1_scales[:, g, :], w1_grouped[:, g])
+
+        def small_weights():
+            b1_t = ps_z.tile([P, P], BF16, tag="z_acc", name="b1_t")
+            nc.tensor.transpose(b1_t[:], bias_rows[:], ident_bf[:])
+            nc.vector.tensor_copy(out=b1_cols[:], in_=b1_t[:, 0:F_TILES])
+            b2_all = ps_z.tile([P, FEATURES], F32, tag="z_acc", name="b2_all")
+            nc.tensor.matmul(b2_all[:], lhsT=b2_select[:], rhs=bias_rows[:], start=True, stop=True)
+            nc.vector.tensor_copy(out=b2_f[:], in_=b2_all[:])
+            regroup(nc.vector.tensor_copy, w2_grouped[:], w2_raw[:])
+            quantise(w2_words[:], w2_scales[:], w2_grouped[:])
 
         def at(stage, s, *more):
             if 0 <= s < GROUPS:
@@ -397,6 +414,12 @@ def tile_spatialmemorymodule_pb_kernel(tc, z, Wq1, bq1, Wq2, bq2, out_0, out_1):
                     transposes(i * TILES + n + AHEAD)
                 if i < GROUPS and 1 <= n <= TURNED:
                     turn_back(i, order[n - 1])
+                if i == 0 and n < PASSES:
+                    regroup_weights(n)
+                elif i == 0:
+                    quantise_weights(n - PASSES)
+            if i == 0:
+                small_weights()
             at(project, i - 3)
             at(centre_and_store, i - 4)
 

@@ -118,7 +118,7 @@ def tile_spatialmemorymodule_pb_kernel(tc, z, Wq1, bq1, Wq2, bq2, out_0, out_1):
         )
         ident_f = const.tile([P, P], F32)
         make_identity(nc, ident_f[:])
-        moments = const.tile([P, GROUPS * TILES, 2], F32)
+        all_moments = const.tile([P, GROUPS * TILES, 3], F32)
         var_all = const.tile([P, P], F32)
         nc.vector.memset(var_all[:], 0.0)
         one_col = const.tile([P, 1], F32)
@@ -322,23 +322,23 @@ def tile_spatialmemorymodule_pb_kernel(tc, z, Wq1, bq1, Wq2, bq2, out_0, out_1):
                 in1=b2_f[:].unsqueeze(1).to_broadcast([P, TILES, FEATURES]),
                 op=ALU.add,
             )
-            stats = small.tile([P, TILES, 6], F32, name="stats")
-            for i in range(TILES):
-                nc.vector.bn_stats(out=stats[:, i, :], in_=zq[:, i, :])
-            mean_var = moments[:, s * TILES : (s + 1) * TILES, :]
-            for i in range(TILES):
-                nc.vector.bn_aggr(out=mean_var[:, i, :], in_=stats[:, i, :])
-            live["zq", s] = (zq, mean_var)
+            moments = all_moments[:, s * TILES : (s + 1) * TILES, :]
+            for i in range(0, TILES, 2):
+                nc.vector.bn_stats(
+                    out=moments[:, i : i + 2, :].rearrange("p i m -> p (i m)"),
+                    in_=zq[:, i : i + 2, :].rearrange("p i d -> p d i"),
+                )
+            live["zq", s] = (zq, moments)
 
         def centre_and_store(s):
-            zq, mean_var = live.pop(("zq", s))
+            zq, moments = live.pop(("zq", s))
             inv_length = small.tile([P, TILES], F32, name="inv_length")
-            inverse_root(inv_length[:], mean_var[:, :, 1], float(FEATURES), TILES)
+            inverse_root(inv_length[:], moments[:, :, 2], 1.0, TILES)
             engine = nc.vector if s == GROUPS - 1 else nc.gpsimd
             minus_mean = small.tile([P, TILES], F32, name="minus_mean")
             engine.tensor_scalar(
                 out=minus_mean[:],
-                in0=mean_var[:, :, 0],
+                in0=moments[:, :, 1],
                 scalar1=-1.0,
                 scalar2=0.0,
                 op0=ALU.mult,
@@ -429,10 +429,10 @@ def tile_spatialmemorymodule_pb_kernel(tc, z, Wq1, bq1, Wq2, bq2, out_0, out_1):
                     out=var_all[:, 0 : GROUPS * TILES].rearrange("p (b k) -> p b k", b=BATCH)[
                         :, :, place : place + count
                     ],
-                    in0=moments[:].rearrange("p (b y k) m -> p y b k m", b=BATCH, y=GROUPS_PER_IMAGE)[
-                        :, y, :, first : first + count, 1
-                    ],
-                    scalar1=FEATURES / (FEATURES - 1.0),
+                    in0=all_moments[:].rearrange(
+                        "p (b y k) m -> p y b k m", b=BATCH, y=GROUPS_PER_IMAGE
+                    )[:, y, :, first : first + count, 2],
+                    scalar1=1.0 / (FEATURES - 1.0),
                     scalar2=None,
                     op0=ALU.mult,
                 )

from contextlib import ExitStack

import concourse.mybir as mybir
from concourse.masks import make_identity

BF16 = mybir.dt.bfloat16
F32 = mybir.dt.float32
U32 = mybir.dt.uint32
U8 = mybir.dt.uint8
FP8X4 = mybir.dt.float8_e4m3fn_x4
ACT = mybir.ActivationFunctionType
ALU = mybir.AluOpType

P = 128
PACK = 4
BATCH, CHANNELS, PIXELS = 8, 1024, 1024
HIDDEN, FEATURES = 512, 128
PASSES = CHANNELS // (P * PACK)
F_TILES = HIDDEN // P
GROUP = 512
TILES = GROUP // P
GROUPS = BATCH * PIXELS // GROUP
GROUPS_PER_IMAGE = PIXELS // GROUP
EPS = 1e-12
TINY = 1e-30
B2_ROW = 32
RUN = 4
DIRECT, TURNED = 1, 3
WORD_ROWS = 2
AHEAD = 2
DEEPEST_LAG = 4

FLOPS = 2 * BATCH * PIXELS * (CHANNELS * HIDDEN + HIDDEN * FEATURES)


def tile_spatialmemorymodule_pb_kernel(tc, z, Wq1, bq1, Wq2, bq2, out_0, out_1):
    nc = tc.nc
    with ExitStack() as ctx:
        const = ctx.enter_context(tc.tile_pool(name="const", bufs=1))
        xpool = ctx.enter_context(tc.tile_pool(name="xpool", bufs=BATCH))
        work = ctx.enter_context(tc.tile_pool(name="work", bufs=2))
        late = ctx.enter_context(tc.tile_pool(name="late", bufs=3))
        small = ctx.enter_context(tc.tile_pool(name="small", bufs=4))
        ps_t = ctx.enter_context(tc.psum_pool(name="ps_t", bufs=3))
        ps_b = ctx.enter_context(tc.psum_pool(name="ps_b", bufs=1))
        ps_r = ctx.enter_context(tc.psum_pool(name="ps_r", bufs=1))
        ps_h = ctx.enter_context(tc.psum_pool(name="ps_h", bufs=2))
        ps_z = ctx.enter_context(tc.psum_pool(name="ps_z", bufs=1))

        def regroup(engine_copy, dst, src):
            engine_copy(
                out=dst.rearrange("p (c i) t -> p c t i", i=RUN),
                in_=src.rearrange("p t (c i) -> p c t i", i=RUN),
            )

        def quantise(words, scales, grouped):
            nc.vector.quantize_mx(
                out=words.bitcast(FP8X4), scales=scales, in_=grouped.rearrange("p c t -> p (c t)")
            )

        x_direct, x_turned = {}, {}

        def load_image(image, pieces):
            split = GROUPS_PER_IMAGE * DIRECT * P
            xt = xpool.tile([P, PASSES * PACK, PIXELS - split], BF16, name="xt")
            xd = xpool.tile([P, PASSES, PACK, split], BF16, name="xd")
            from_turned = z[image].rearrange("(a p) h w -> p a (h w)", p=P)[:, :, split:]
            from_direct = z[image].rearrange("(g p j) h w -> p g j (h w)", g=PASSES, j=PACK)
            d, t = split // pieces, (PIXELS - split) // pieces
            for i in range(pieces):
                nc.sync.dma_start(
                    out=xt[:, :, i * t : (i + 1) * t], in_=from_turned[:, :, i * t : (i + 1) * t]
                )
                for g in range(PASSES):
                    nc.sync.dma_start(
                        out=xd[:, g, :, i * d : (i + 1) * d],
                        in_=from_direct[:, g, :, i * d : (i + 1) * d],
                    )
                if image == 0:
                    (load_biases, load_weights)[i]()
            for y in range(GROUPS_PER_IMAGE):
                x_turned[image * GROUPS_PER_IMAGE + y] = xt[:, :, y * TURNED * P : (y + 1) * TURNED * P]
                x_direct[image * GROUPS_PER_IMAGE + y] = xd[:, :, :, y * DIRECT * P : (y + 1) * DIRECT * P]

        bias_rows = const.tile([P, P], BF16)
        nc.vector.memset(bias_rows[:], 0.0)
        b2_select = const.tile([P, P], BF16)
        nc.vector.memset(b2_select[:], 0.0)
        nc.vector.memset(b2_select[B2_ROW : B2_ROW + 1, :], 1.0)
        w2_raw = const.tile([P, PACK, FEATURES], BF16)
        w1_raw = const.tile([P, PASSES, PACK, HIDDEN], BF16)

        def load_biases():
            nc.sync.dma_start(
                out=bias_rows[0:F_TILES, :], in_=bq1.rearrange("(t p) -> t p", p=P)
            )
            nc.sync.dma_start(
                out=bias_rows[B2_ROW : B2_ROW + 1, :], in_=bq2.rearrange("(o d) -> o d", o=1)
            )

        def load_weights():
            nc.sync.dma_start(out=w2_raw[:], in_=Wq2.rearrange("(t p) d -> p t d", p=P))
            nc.sync.dma_start(
                out=w1_raw[:].rearrange("p g j f -> p g (j f)"),
                in_=Wq1.rearrange("(g p j) f -> p g (j f)", g=PASSES, j=PACK),
            )

        load_image(0, GROUPS_PER_IMAGE)
        for image in range(1, BATCH):
            load_image(image, 1)

        ident_bf = const.tile([P, P], BF16)
        make_identity(nc, ident_bf[:])
        pairs_bf = const.tile([P, P], BF16)
        nc.gpsimd.tensor_copy(
            out=pairs_bf[:].rearrange("k (u p e) -> k p u e", u=WORD_ROWS, e=2),
            in_=ident_bf[:].rearrange("k (p u e) -> k p u e", u=WORD_ROWS, e=2),
        )
        ident_f = const.tile([P, P], F32)
        make_identity(nc, ident_f[:])
        all_moments = const.tile([P, GROUPS * TILES, 3], F32)
        var_all = const.tile([P, P], F32)
        nc.vector.memset(var_all[:], 0.0)
        one_col = const.tile([P, 1], F32)
        nc.vector.memset(one_col[:], 1.0)
        tiny = const.tile([P, 1], F32)
        nc.vector.tensor_scalar(
            out=tiny[:], in0=one_col[:], scalar1=TINY, scalar2=None, op0=ALU.mult
        )
        table_call = const.tile([P, 1], F32)
        nc.scalar.activation(out=table_call[:], in_=one_col[:], func=ACT.Abs_reciprocal_sqrt)

        live = {}

        order = list(range(DIRECT, TILES)) + list(range(DIRECT))

        def transposes(q):
            s, k = q // TILES, order[q % TILES]
            if k < DIRECT:
                gram = ps_r.tile([P, P], F32, tag="inv_row", name="gram")
                cols = slice(k * P, (k + 1) * P)
                for g in range(PASSES):
                    for j in range(PACK):
                        nc.tensor.matmul(
                            gram[:],
                            lhsT=x_direct[s][:, g, j, cols],
                            rhs=x_direct[s][:, g, j, cols],
                            start=(g == 0 and j == 0),
                            stop=(g == PASSES - 1 and j == PACK - 1),
                        )
                live["x_t", s, k] = gram
                return
            x_t = ps_t.tile([P, PASSES, WORD_ROWS, PACK, P // 2], BF16, name="x_t")
            for g in range(PASSES):
                for j in range(PACK):
                    nc.tensor.transpose(
                        x_t[:, g, :, j, :],
                        x_turned[s][:, g * PACK + j, (k - DIRECT) * P : (k - DIRECT + 1) * P],
                        pairs_bf[:],
                    )
            live["x_t", s, k] = x_t

        def squares(q):
            s, k = q // TILES, order[q % TILES]
            if q % TILES == 0:
                live["norm_sq", s] = small.tile([P, TILES], F32, name="norm_sq")
                live["inv_norm", s] = small.tile([P, TILES], F32, name="inv_norm")
            if k < DIRECT:
                masked = work.tile([P, P], F32, name="masked")
                nc.vector.scalar_tensor_tensor(
                    out=masked[:],
                    in0=live.pop(("x_t", s, k))[:],
                    scalar=1.0,
                    in1=ident_f[:],
                    op0=ALU.mult,
                    op1=ALU.mult,
                    accum_out=live["norm_sq", s][:, k : k + 1],
                )
                return
            x_t = live["x_t", s, k]
            unused = work.tile([P, CHANNELS], BF16, name="unused")
            nc.scalar.activation(
                out=unused[:],
                in_=x_t[:].rearrange("p g u b c -> p (g u b c)"),
                func=ACT.Square,
                accum_out=live["norm_sq", s][:, k : k + 1],
            )

        def inverse_root(out, in_, scale, width):
            inverse = small.tile([P, TILES], F32, name="inverse")
            nc.scalar.activation(
                out=inverse[:, 0:width],
                in_=in_,
                func=ACT.Abs_reciprocal_sqrt,
                scale=scale,
                bias=tiny[:],
            )
            nc.vector.tensor_scalar(
                out=out, in0=inverse[:, 0:width], scalar1=1.0 / EPS, scalar2=None, op0=ALU.min
            )

        def inverse_norm(s, k):
            one = slice(k, k + 1)
            inverse_root(live["inv_norm", s][:, one], live["norm_sq", s][:, one], 1.0, 1)

        def grouped_tile(s):
            if ("grouped_x", s) not in live:
                live["grouped_x", s] = work.tile(
                    [P, PASSES, GROUP, PACK], BF16, name="grouped_x", align_bytes=64
                )
            return live["grouped_x", s]

        def scale_turned(s, k):
            x_t = live.pop(("x_t", s, k))
            xn = work.tile([P, PASSES, WORD_ROWS, 2 * P], BF16, name="xn")
            nc.vector.tensor_scalar(
                out=xn[:].rearrange("p g u c -> p (g u c)"),
                in0=x_t[:].rearrange("p g u b c -> p (g u b c)"),
                scalar1=live["inv_norm", s][:, k : k + 1],
                scalar2=None,
                op0=ALU.mult,
            )
            live["xn", s, k] = xn

        def turn_back(s, k):
            xn = live.pop(("xn", s, k))
            x_b = ps_b.tile([P, PASSES, WORD_ROWS, P], F32, name="x_b")
            for g in range(PASSES):
                for u in range(WORD_ROWS):
                    nc.tensor.transpose(x_b[:, g, u, :], xn[:, g, u, :].bitcast(F32), ident_f[:])
            words = grouped_tile(s)[:, :, k * P : (k + 1) * P, :].bitcast(F32)
            nc.scalar.copy(out=words, in_=x_b[:].rearrange("p g u n -> p g n u"))

        def spread_inverse_norms(s):
            inv_norm = live["inv_norm", s]
            inv_row = ps_r.tile([P, DIRECT * P], F32, name="inv_row")
            for i in range(DIRECT):
                nc.tensor.transpose(
                    inv_row[:, i * P : (i + 1) * P],
                    inv_norm[:, i : i + 1].to_broadcast([P, P]),
                    ident_f[:],
                )
            live["inv_row", s] = inv_row

        def normalise(s):
            inv_row = live.pop(("inv_row", s))
            grouped_x = grouped_tile(s)
            for g in range(PASSES):
                nc.vector.tensor_tensor(
                    out=grouped_x[:, g, 0 : DIRECT * P].rearrange("p (c i) t -> p c t i", i=RUN),
                    in0=x_direct[s][:, g].rearrange("p t (c i) -> p c t i", i=RUN),
                    in1=inv_row[:]
                    .rearrange("p (c i) -> p c i", i=RUN)
                    .unsqueeze(2)
                    .to_broadcast([P, DIRECT * P // RUN, PACK, RUN]),
                    op=ALU.mult,
                )

        def quantise_x(s):
            grouped_x = live.pop(("grouped_x", s))
            x_words = work.tile([P, PASSES, GROUP], U32, name="x_words", align_bytes=64)
            x_scales = work.tile([P, PASSES, GROUP], U8, name="x_scales", align_bytes=64)
            for g in range(PASSES):
                quantise(x_words[:, g, :], x_scales[:, g, :], grouped_x[:, g])
            live["x", s] = (x_words, x_scales)

        def hidden(s, t):
            if t == 0:
                live["h_planes", s] = work.tile([P, F_TILES, GROUP], BF16, name="h_planes")
            x_words, x_scales = live["x", s]
            f_cols = slice(t * P, (t + 1) * P)
            h_acc = ps_h.tile([P, GROUP], F32, name="h_acc")
            for g in range(PASSES):
                nc.tensor.matmul_mx(
                    out=h_acc[:],
                    lhsT=w1_words[:, g, f_cols].bitcast(FP8X4),
                    lhsT_scale=w1_scales[:, g, f_cols],
                    rhs=x_words[:, g, :].bitcast(FP8X4),
                    rhs_scale=x_scales[:, g, :],
                    start=(g == 0),
                    stop=(g == PASSES - 1),
                )
            nc.scalar.activation(
                out=live["h_planes", s][:, t, :],
                in_=h_acc[:],
                func=ACT.Relu,
                bias=b1_cols[:, t : t + 1],
            )

        def regroup_h(s):
            grouped_h = work.tile([P, GROUP, PACK], BF16, name="grouped_h", align_bytes=64)
            regroup(nc.vector.tensor_copy, grouped_h[:], live.pop(("h_planes", s))[:])
            live["grouped_h", s] = grouped_h

        def quantise_h(s):
            h_words = work.tile([P, GROUP], U32, name="h_words", align_bytes=64)
            h_scales = work.tile([P, GROUP], U8, name="h_scales", align_bytes=64)
            quantise(h_words[:], h_scales[:], live.pop(("grouped_h", s))[:])
            live["h", s] = (h_words, h_scales)

        def project(s):
            h_words, h_scales = live.pop(("h", s))
            z_acc = ps_z.tile([P, TILES, FEATURES], F32, name="z_acc")
            for i in range(TILES):
                rows = slice(i * P, (i + 1) * P)
                nc.tensor.matmul_mx(
                    out=z_acc[:, i, :],
                    lhsT=h_words[:, rows].bitcast(FP8X4),
                    lhsT_scale=h_scales[:, rows],
                    rhs=w2_words[:].bitcast(FP8X4),
                    rhs_scale=w2_scales[:],
                    start=True,
                    stop=True,
                )
            live["z_acc", s] = z_acc

        def statistics(s):
            zq = late.tile([P, TILES, FEATURES], F32, name="zq")
            nc.vector.tensor_tensor(
                out=zq[:],
                in0=live.pop(("z_acc", s))[:],
                in1=b2_f[:].unsqueeze(1).to_broadcast([P, TILES, FEATURES]),
                op=ALU.add,
            )
            moments = all_moments[:, s * TILES : (s + 1) * TILES, :]
            for i in range(0, TILES, 2):
                nc.vector.bn_stats(
                    out=moments[:, i : i + 2, :].rearrange("p i m -> p (i m)"),
                    in_=zq[:, i : i + 2, :].rearrange("p i d -> p d i"),
                )
            live["zq", s] = (zq, moments)

        def centre_and_store(s):
            zq, moments = live.pop(("zq", s))
            inv_length = small.tile([P, TILES], F32, name="inv_length")
            inverse_root(inv_length[:], moments[:, :, 2], 1.0, TILES)
            engine = nc.vector if s == GROUPS - 1 else nc.gpsimd
            minus_mean = small.tile([P, TILES], F32, name="minus_mean")
            engine.tensor_scalar(
                out=minus_mean[:],
                in0=moments[:, :, 1],
                scalar1=-1.0,
                scalar2=0.0,
                op0=ALU.mult,
                op1=ALU.add,
            )
            zc = late.tile([P, TILES, FEATURES], F32, name="zc")
            for i in range(TILES):
                engine.tensor_scalar(
                    out=zc[:, i, :],
                    in0=zq[:, i, :],
                    scalar1=minus_mean[:, i : i + 1],
                    scalar2=inv_length[:, i : i + 1],
                    op0=ALU.add,
                    op1=ALU.mult,
                )
            image, y = divmod(s, GROUPS_PER_IMAGE)
            tile_0 = image * GROUPS_PER_IMAGE * TILES + y * DIRECT
            tile_1 = image * GROUPS_PER_IMAGE * TILES + GROUPS_PER_IMAGE * DIRECT + y * TURNED
            for tile, k, count in ((tile_0, 0, DIRECT), (tile_1, DIRECT, TURNED)):
                nc.sync.dma_start(
                    out=out_0[tile * P : (tile + count) * P, :].rearrange("(i p) d -> p i d", p=P),
                    in_=zc[:, k : k + count],
                )

        for q in range(AHEAD):
            transposes(q)

        b2_f = const.tile([P, FEATURES], F32)
        w2_grouped = const.tile([P, FEATURES, PACK], BF16, align_bytes=64)
        w1_grouped = const.tile([P, PASSES, HIDDEN, PACK], BF16, align_bytes=64)
        w2_words = const.tile([P, FEATURES], U32, align_bytes=64)
        w2_scales = const.tile([P, FEATURES], U8, align_bytes=64)
        w1_words = const.tile([P, PASSES, HIDDEN], U32, align_bytes=64)
        w1_scales = const.tile([P, PASSES, HIDDEN], U8, align_bytes=64)
        b1_cols = const.tile([P, F_TILES], F32)

        def regroup_weights(g):
            regroup(nc.vector.tensor_copy, w1_grouped[:, g], w1_raw[:, g])

        def quantise_weights(g):
            quantise(w1_words[:, g, :], w1_scales[:, g, :], w1_grouped[:, g])

        def small_weights():
            b1_t = ps_z.tile([P, P], BF16, tag="z_acc", name="b1_t")
            nc.tensor.transpose(b1_t[:], bias_rows[:], ident_bf[:])
            nc.vector.tensor_copy(out=b1_cols[:], in_=b1_t[:, 0:F_TILES])
            b2_all = ps_z.tile([P, FEATURES], F32, tag="z_acc", name="b2_all")
            nc.tensor.matmul(b2_all[:], lhsT=b2_select[:], rhs=bias_rows[:], start=True, stop=True)
            nc.vector.tensor_copy(out=b2_f[:], in_=b2_all[:])
            regroup(nc.vector.tensor_copy, w2_grouped[:], w2_raw[:])
            quantise(w2_words[:], w2_scales[:], w2_grouped[:])

        def at(stage, s, *more):
            if 0 <= s < GROUPS:
                stage(s, *more)

        for i in range(GROUPS + DEEPEST_LAG + 1):
            at(spread_inverse_norms, i - 1)
            at(regroup_h, i - 3)
            at(statistics, i - 4)
            at(quantise_h, i - 3)
            at(normalise, i - 1)
            at(quantise_x, i - 1)
            for n in range(TILES):
                if i < GROUPS:
                    k = order[n]
                    squares(i * TILES + n)
                    inverse_norm(i, k)
                    if k >= DIRECT:
                        scale_turned(i, k)
                at(hidden, i - 2, n)
                if i * TILES + n + AHEAD < GROUPS * TILES:
                    transposes(i * TILES + n + AHEAD)
                if i < GROUPS and 1 <= n <= TURNED:
                    turn_back(i, order[n - 1])
                if i == 0 and n < PASSES:
                    regroup_weights(n)
                elif i == 0:
                    quantise_weights(n - PASSES)
            if i == 0:
                small_weights()
            at(project, i - 3)
            at(centre_and_store, i - 4)

        for y in range(GROUPS_PER_IMAGE):
            for first, count, place in ((0, DIRECT, y * DIRECT), (DIRECT, TURNED, GROUPS_PER_IMAGE * DIRECT + y * TURNED)):
                nc.vector.tensor_scalar(
                    out=var_all[:, 0 : GROUPS * TILES].rearrange("p (b k) -> p b k", b=BATCH)[
                        :, :, place : place + count
                    ],
                    in0=all_moments[:].rearrange(
                        "p (b y k) m -> p y b k m", b=BATCH, y=GROUPS_PER_IMAGE
                    )[:, y, :, first : first + count, 2],
                    scalar1=1.0 / (FEATURES - 1.0),
                    scalar2=None,
                    op0=ALU.mult,
                )
        var_t = ps_z.tile([P, P], F32, tag="z_acc")
        nc.tensor.transpose(var_t[:], var_all[:], ident_f[:])
        var_rows = const.tile([P, P], F32)
        nc.vector.tensor_copy(out=var_rows[:], in_=var_t[:])
        nc.sync.dma_start(
            out=out_1.rearrange("(c p) o -> c (p o)", p=P), in_=var_rows[0 : GROUPS * TILES, :]
        )
